import numpy as np
import ml_dtypes


def mxq(x, axis, fmt="e4m3"):
    dtype, down = {"e4m3": (ml_dtypes.float8_e4m3fn, 7), "e5m2": (ml_dtypes.float8_e5m2, 14)}[fmt]
    v = np.moveaxis(np.asarray(x, np.float32).astype(ml_dtypes.bfloat16).astype(np.float64), axis, -1)
    blocks = v.reshape(v.shape[:-1] + (-1, 32))
    amax = np.abs(blocks).max(-1, keepdims=True)
    byte = np.maximum(np.where(amax > 0, np.frexp(amax)[1] - 1 + 127, 0) - down, 1)
    scale = np.exp2(byte - 127.0)
    codes = (blocks / scale).astype(np.float32).astype(dtype).astype(np.float64)
    return np.moveaxis((codes * scale).reshape(v.shape), -1, axis)


WIDE = False


def mx_kscale(k):
    if not WIDE:
        return np.ones(k)
    levels = np.array([10, -10, 5, -5, 0])
    a = np.random.permutation(np.resize(levels, k // 512 * 4)).reshape(k // 512, 4)
    idx = np.arange(k)
    return np.exp2(a[idx // 512, idx % 128 // 32])


BF16 = ml_dtypes.bfloat16


def bf(x):
    return np.asarray(x, np.float32).astype(BF16)


def f64(x):
    return np.asarray(x).astype(np.float64)


N, G, GIN, GOUT = 1024, 8, 512, 512

P0 = np.array([0.5, 1.0, 0.5, 0.3])
Q0 = np.array([0.5, 0.3, 0.2])


def rational(y, p, q):
    p = p[None, :, :, None]
    q = q[None, :, :, None]
    y2 = y * y
    y3 = y2 * y
    num = p[:, :, 0] + p[:, :, 1] * y + p[:, :, 2] * y2 + p[:, :, 3] * y3
    den = 1.0 + np.abs(q[:, :, 0] * y + q[:, :, 1] * y2 + q[:, :, 2] * y3)
    return num / den


def setup_inputs():
    s = mx_kscale(GIN)
    return {"x": bf(np.random.standard_normal((N, G * GIN)) * np.tile(s, G)),
            "W": bf(np.random.standard_normal((G, GIN, GOUT)) / np.sqrt(GIN) / s[None, :, None]),
            "b": bf(np.random.standard_normal((G, GOUT)) * 0.3),
            "p": bf(P0 + 0.1 * np.random.standard_normal((G, P0.size))),
            "q": bf(Q0 + 0.05 * np.random.standard_normal((G, Q0.size)))}


def reference(x, W, b, p, q):
    n = x.shape[0]
    xg = f64(x).reshape(n, G, GIN)
    xq = mxq(xg, 2, "e4m3")
    wq = mxq(f64(W), 1, "e4m3")
    y = (xq.transpose(1, 0, 2) @ wq).transpose(1, 0, 2) + f64(b)[None]
    out = rational(y, f64(p), f64(q))
    return out.reshape(n, G * GOUT)

@@ -1,0 +1,210 @@
+from contextlib import ExitStack
+
+import concourse.mybir as mybir
+from concourse.masks import make_identity
+
+F32 = mybir.dt.float32
+BF16 = mybir.dt.bfloat16
+U32 = mybir.dt.uint32
+U8 = mybir.dt.uint8
+FP8X4 = mybir.dt.float8_e4m3fn_x4
+AF = mybir.ActivationFunctionType
+ALU = mybir.AluOpType
+
+P = 128
+N_ROWS, G, GIN, GOUT = 1024, 8, 512, 512
+HALF = 512
+OB = GOUT // P
+NBH = HALF // P
+FLOPS = 2 * N_ROWS * G * GIN * GOUT
+
+
+def tile_groupkanlayer_kernel(tc, x, W, b, p, q, out):
+    nc = tc.nc
+    with ExitStack() as ctx:
+        const = ctx.enter_context(tc.tile_pool(name="const", bufs=1))
+        inp = ctx.enter_context(tc.tile_pool(name="inp", bufs=2))
+        grp = ctx.enter_context(tc.tile_pool(name="grp", bufs=2))
+        qnt = ctx.enter_context(tc.tile_pool(name="qnt", bufs=2))
+        ep = ctx.enter_context(tc.tile_pool(name="ep", bufs=2))
+        accp = ctx.enter_context(tc.psum_pool(name="accp", bufs=4))
+        tpp = ctx.enter_context(tc.psum_pool(name="tpp", bufs=4))
+
+        one = const.tile([P, 1], F32, name="one")
+        nc.vector.memset(one[:], 1.0)
+        warm = const.tile([P, 1], F32, name="warm")
+        nc.scalar.activation(out=warm[:], in_=one[:], func=AF.Abs_reciprocal_sqrt)
+        ident = const.tile([P, P], F32, name="ident")
+        make_identity(nc, ident[:])
+
+        bz = const.tile([P, P], BF16, name="bz")
+        nc.vector.memset(bz[:], 0.0)
+        nc.scalar.dma_start(out=bz[0 : G * OB, :], in_=b.rearrange("g (ob o) -> (g ob) o", o=P))
+        pq = const.tile([P, 64], BF16, name="pq")
+        nc.scalar.dma_start(out=pq[:, 0:32], in_=p.rearrange("g c -> (g c)").partition_broadcast(P))
+        nc.scalar.dma_start(out=pq[:, 32:56], in_=q.rearrange("g c -> (g c)").partition_broadcast(P))
+
+        slabs = {}
+        quant = {}
+        work = {}
+
+        def load(g):
+            xs = inp.tile([P, 2 * NBH, GIN], BF16, name="xs")
+            for h in range(2):
+                nc.sync.dma_start(
+                    out=xs[:, h * NBH : (h + 1) * NBH, :],
+                    in_=x[h * HALF : (h + 1) * HALF, g * GIN : (g + 1) * GIN].rearrange("(nb r) c -> r nb c", r=P),
+                )
+                if h == 0:
+                    wt = inp.tile([P, 4, GOUT], BF16, name="wt")
+                    nc.sync.dma_start(
+                        out=wt[:].rearrange("k (u e) c -> k u (e c)", u=2),
+                        in_=W[g].rearrange("(u k e) c -> k u (e c)", u=2, e=2),
+                    )
+            gx = grp.tile([P, 4 * N_ROWS], BF16, name="gx", align_bytes=64)
+            xq = qnt.tile([P, N_ROWS], U32, name="xq", align_bytes=64)
+            xsc = qnt.tile([P, N_ROWS], U8, name="xsc", align_bytes=64)
+            wq = qnt.tile([P, GOUT], U32, name="wq", align_bytes=64)
+            wsc = qnt.tile([P, GOUT], U8, name="wsc", align_bytes=64)
+            slabs[g] = (xs, wt, gx)
+            quant[g] = (xq, xsc, wq, wsc)
+
+        def prep_w(g):
+            wt = slabs[g][1]
+            wq, wsc = quant[g][2], quant[g][3]
+            gw = grp.tile([P, GOUT, 4], BF16, name="gw", align_bytes=64)
+            nc.scalar.copy(out=gw[:], in_=wt[:].rearrange("k t o -> k o t"))
+            nc.vector.quantize_mx(out=wq[:].bitcast(FP8X4), scales=wsc[:], in_=gw[:].rearrange("k o t -> k (o t)"))
+
+        def prep_x(g, h):
+            xs, gx = slabs[g][0], slabs[g][2]
+            xq, xsc = quant[g][0], quant[g][1]
+            xf = xs[:].bitcast(F32)
+            gxf = gx[:].bitcast(F32).rearrange("k (n u) -> k n u", u=2)
+            for j in range(2):
+                xt = tpp.tile([P, 2, 2 * P], F32, name="xt", tag="tp")
+                for k in range(2):
+                    nb = h * NBH + 2 * j + k
+                    for u in range(2):
+                        nc.tensor.transpose(
+                            out=xt[:, u, k * P : (k + 1) * P], in_=xf[:, nb, u * P : (u + 1) * P], identity=ident[:]
+                        )
+                n0 = h * HALF + j * 2 * P
+                nc.scalar.copy(out=gxf[:, n0 : n0 + 2 * P, :], in_=xt[:].rearrange("k u n -> k n u"))
+            nc.vector.quantize_mx(
+                out=xq[:, h * HALF : (h + 1) * HALF].bitcast(FP8X4),
+                scales=xsc[:, h * HALF : (h + 1) * HALF],
+                in_=gx[:, h * 4 * HALF : (h + 1) * 4 * HALF],
+            )
+
+        def front(u):
+            g, h = divmod(u, 2)
+            xq, xsc, wq, wsc = quant[g]
+            z = ep.tile([P, OB, HALF], F32, name="z")
+            e1 = ep.tile([P, OB, HALF], F32, name="e1")
+            e2 = ep.tile([P, OB, HALF], F32, name="e2")
+            nn = ep.tile([P, OB, HALF], F32, name="nn")
+            dd = ep.tile([P, OB, HALF], F32, name="dd")
+            work[u] = (nn, dd)
+            accs = []
+            for ob in range(OB):
+                acc = accp.tile([P, HALF], F32, name="acc")
+                nc.tensor.matmul_mx(
+                    out=acc[:],
+                    lhsT=wq[:, ob * P : (ob + 1) * P].bitcast(FP8X4),
+                    lhsT_scale=wsc[:, ob * P : (ob + 1) * P],
+                    rhs=xq[:, h * HALF : (h + 1) * HALF].bitcast(FP8X4),
+                    rhs_scale=xsc[:, h * HALF : (h + 1) * HALF],
+                    start=True,
+                    stop=True,
+                )
+                accs.append(acc)
+            for ob in range(OB):
+                bcol = bT[:, g * OB + ob : g * OB + ob + 1]
+                nc.scalar.activation(out=z[:, ob, :], in_=accs[ob][:], func=AF.Square, bias=bcol, scale=1.0)
+            for j in range(2):
+                s = slice(2 * j, 2 * j + 2)
+                nc.gpsimd.tensor_scalar(
+                    out=e1[:, s, :], in0=z[:, s, :], scalar1=pc(g, 3), scalar2=pc(g, 1), op0=ALU.mult, op1=ALU.add
+                )
+                nc.gpsimd.tensor_scalar(
+                    out=e2[:, s, :], in0=z[:, s, :], scalar1=qc(g, 2), scalar2=qc(g, 0), op0=ALU.mult, op1=ALU.add
+                )
+            for ob in range(OB):
+                bcol = bT[:, g * OB + ob : g * OB + ob + 1]
+                nc.vector.scalar_tensor_tensor(
+                    out=nn[:, ob, :], in0=accs[ob][:], scalar=bcol, in1=e1[:, ob, :], op0=ALU.add, op1=ALU.mult
+                )
+                nc.vector.scalar_tensor_tensor(
+                    out=dd[:, ob, :], in0=accs[ob][:], scalar=bcol, in1=e2[:, ob, :], op0=ALU.add, op1=ALU.mult
+                )
+            nc.vector.scalar_tensor_tensor(
+                out=dd[:], in0=z[:], scalar=qc(g, 1), in1=dd[:], op0=ALU.mult, op1=ALU.add
+            )
+            nc.vector.scalar_tensor_tensor(
+                out=nn[:], in0=z[:], scalar=pc(g, 2), in1=nn[:], op0=ALU.mult, op1=ALU.add
+            )
+
+        def mid(u):
+            dd = work[u][1]
+            nc.scalar.activation(out=dd[:], in_=dd[:], func=AF.Abs)
+            nc.scalar.activation(out=dd[:], in_=dd[:], func=AF.Abs_reciprocal_sqrt, bias=one[:], scale=1.0)
+
+        def back(u):
+            g, h = divmod(u, 2)
+            nn, dd = work[u]
+            rr = ep.tile([P, NBH, GOUT], F32, name="rr")
+            oo = ep.tile([P, NBH, GOUT], F32, name="oo")
+            for nb in range(NBH):
+                tw = tpp.tile([P, GOUT], F32, name="tw", tag="tp")
+                tn = tpp.tile([P, GOUT], F32, name="tn", tag="tp")
+                for ob in range(OB):
+                    nc.tensor.transpose(
+                        out=tw[:, ob * P : (ob + 1) * P], in_=dd[:, ob, nb * P : (nb + 1) * P], identity=ident[:]
+                    )
+                for ob in range(OB):
+                    nc.tensor.transpose(
+                        out=tn[:, ob * P : (ob + 1) * P], in_=nn[:, ob, nb * P : (nb + 1) * P], identity=ident[:]
+                    )
+                nc.scalar.activation(out=rr[:, nb, :], in_=tw[:], func=AF.Square)
+                nc.vector.scalar_tensor_tensor(
+                    out=oo[:, nb, :], in0=tn[:], scalar=pc(g, 0), in1=rr[:, nb, :], op0=ALU.add, op1=ALU.mult
+                )
+                r0 = h * HALF + nb * P
+                nc.sync.dma_start(out=out[r0 : r0 + P, g * GOUT : (g + 1) * GOUT], in_=oo[:, nb, :])
+
+        load(0)
+        load(1)
+
+        bzf = const.tile([P, P], F32, name="bzf")
+        nc.vector.tensor_copy(out=bzf[:], in_=bz[:])
+        bps = tpp.tile([P, GOUT], F32, name="bps", tag="tp")
+        nc.tensor.transpose(out=bps[:, 0:P], in_=bzf[:], identity=ident[:])
+        bT = const.tile([P, G * OB], F32, name="bT")
+        nc.vector.tensor_copy(out=bT[:], in_=bps[:, 0 : G * OB])
+        cf = const.tile([P, 56], F32, name="cf")
+        nc.vector.tensor_copy(out=cf[:], in_=pq[:, 0:56])
+
+        def pc(g, j):
+            return cf[:, 4 * g + j : 4 * g + j + 1]
+
+        def qc(g, j):
+            return cf[:, 32 + 3 * g + j : 32 + 3 * g + j + 1]
+
+        prep_w(0)
+        prep_x(0, 0)
+        prep_x(0, 1)
+        n_units = 2 * G
+        for u in range(n_units):
+            g, h = divmod(u, 2)
+            front(u)
+            if u >= 1:
+                back(u - 1)
+            mid(u)
+            if g + 1 < G:
+                if h == 0:
+                    if g + 2 < G:
+                        load(g + 2)
+                    prep_w(g + 1)
+                prep_x(g + 1, h)
+        back(n_units - 1)

@@ -30,12 +30,7 @@ def tile_groupkanlayer_kernel(tc, x, W, b, p, q, out):
         accp = ctx.enter_context(tc.psum_pool(name="accp", bufs=4))
         tpp = ctx.enter_context(tc.psum_pool(name="tpp", bufs=4))
 
-        one = const.tile([P, 1], F32, name="one")
-        nc.vector.memset(one[:], 1.0)
-        warm = const.tile([P, 1], F32, name="warm")
-        nc.scalar.activation(out=warm[:], in_=one[:], func=AF.Abs_reciprocal_sqrt)
-        ident = const.tile([P, P], F32, name="ident")
-        make_identity(nc, ident[:])
+        ctx.enter_context(tc.manual_schedule())
 
         bz = const.tile([P, P], BF16, name="bz")
         nc.vector.memset(bz[:], 0.0)
@@ -43,138 +38,12 @@ def tile_groupkanlayer_kernel(tc, x, W, b, p, q, out):
         pq = const.tile([P, 64], BF16, name="pq")
         nc.scalar.dma_start(out=pq[:, 0:32], in_=p.rearrange("g c -> (g c)").partition_broadcast(P))
         nc.scalar.dma_start(out=pq[:, 32:56], in_=q.rearrange("g c -> (g c)").partition_broadcast(P))
-
-        slabs = {}
-        quant = {}
-        work = {}
-
-        def load(g):
-            xs = inp.tile([P, 2 * NBH, GIN], BF16, name="xs")
-            for h in range(2):
-                nc.sync.dma_start(
-                    out=xs[:, h * NBH : (h + 1) * NBH, :],
-                    in_=x[h * HALF : (h + 1) * HALF, g * GIN : (g + 1) * GIN].rearrange("(nb r) c -> r nb c", r=P),
-                )
-                if h == 0:
-                    wt = inp.tile([P, 4, GOUT], BF16, name="wt")
-                    nc.sync.dma_start(
-                        out=wt[:].rearrange("k (u e) c -> k u (e c)", u=2),
-                        in_=W[g].rearrange("(u k e) c -> k u (e c)", u=2, e=2),
-                    )
-            gx = grp.tile([P, 4 * N_ROWS], BF16, name="gx", align_bytes=64)
-            xq = qnt.tile([P, N_ROWS], U32, name="xq", align_bytes=64)
-            xsc = qnt.tile([P, N_ROWS], U8, name="xsc", align_bytes=64)
-            wq = qnt.tile([P, GOUT], U32, name="wq", align_bytes=64)
-            wsc = qnt.tile([P, GOUT], U8, name="wsc", align_bytes=64)
-            slabs[g] = (xs, wt, gx)
-            quant[g] = (xq, xsc, wq, wsc)
-
-        def prep_w(g):
-            wt = slabs[g][1]
-            wq, wsc = quant[g][2], quant[g][3]
-            gw = grp.tile([P, GOUT, 4], BF16, name="gw", align_bytes=64)
-            nc.scalar.copy(out=gw[:], in_=wt[:].rearrange("k t o -> k o t"))
-            nc.vector.quantize_mx(out=wq[:].bitcast(FP8X4), scales=wsc[:], in_=gw[:].rearrange("k o t -> k (o t)"))
-
-        def prep_x(g, h):
-            xs, gx = slabs[g][0], slabs[g][2]
-            xq, xsc = quant[g][0], quant[g][1]
-            xf = xs[:].bitcast(F32)
-            gxf = gx[:].bitcast(F32).rearrange("k (n u) -> k n u", u=2)
-            for j in range(2):
-                xt = tpp.tile([P, 2, 2 * P], F32, name="xt", tag="tp")
-                for k in range(2):
-                    nb = h * NBH + 2 * j + k
-                    for u in range(2):
-                        nc.tensor.transpose(
-                            out=xt[:, u, k * P : (k + 1) * P], in_=xf[:, nb, u * P : (u + 1) * P], identity=ident[:]
-                        )
-                n0 = h * HALF + j * 2 * P
-                nc.scalar.copy(out=gxf[:, n0 : n0 + 2 * P, :], in_=xt[:].rearrange("k u n -> k n u"))
-            nc.vector.quantize_mx(
-                out=xq[:, h * HALF : (h + 1) * HALF].bitcast(FP8X4),
-                scales=xsc[:, h * HALF : (h + 1) * HALF],
-                in_=gx[:, h * 4 * HALF : (h + 1) * 4 * HALF],
-            )
-
-        def front(u):
-            g, h = divmod(u, 2)
-            xq, xsc, wq, wsc = quant[g]
-            z = ep.tile([P, OB, HALF], F32, name="z")
-            e1 = ep.tile([P, OB, HALF], F32, name="e1")
-            e2 = ep.tile([P, OB, HALF], F32, name="e2")
-            nn = ep.tile([P, OB, HALF], F32, name="nn")
-            dd = ep.tile([P, OB, HALF], F32, name="dd")
-            work[u] = (nn, dd)
-            accs = []
-            for ob in range(OB):
-                acc = accp.tile([P, HALF], F32, name="acc")
-                nc.tensor.matmul_mx(
-                    out=acc[:],
-                    lhsT=wq[:, ob * P : (ob + 1) * P].bitcast(FP8X4),
-                    lhsT_scale=wsc[:, ob * P : (ob + 1) * P],
-                    rhs=xq[:, h * HALF : (h + 1) * HALF].bitcast(FP8X4),
-                    rhs_scale=xsc[:, h * HALF : (h + 1) * HALF],
-                    start=True,
-                    stop=True,
-                )
-                accs.append(acc)
-            for ob in range(OB):
-                bcol = bT[:, g * OB + ob : g * OB + ob + 1]
-                nc.scalar.activation(out=z[:, ob, :], in_=accs[ob][:], func=AF.Square, bias=bcol, scale=1.0)
-            for j in range(2):
-                s = slice(2 * j, 2 * j + 2)
-                nc.gpsimd.tensor_scalar(
-                    out=e1[:, s, :], in0=z[:, s, :], scalar1=pc(g, 3), scalar2=pc(g, 1), op0=ALU.mult, op1=ALU.add
-                )
-                nc.gpsimd.tensor_scalar(
-                    out=e2[:, s, :], in0=z[:, s, :], scalar1=qc(g, 2), scalar2=qc(g, 0), op0=ALU.mult, op1=ALU.add
-                )
-            for ob in range(OB):
-                bcol = bT[:, g * OB + ob : g * OB + ob + 1]
-                nc.vector.scalar_tensor_tensor(
-                    out=nn[:, ob, :], in0=accs[ob][:], scalar=bcol, in1=e1[:, ob, :], op0=ALU.add, op1=ALU.mult
-                )
-                nc.vector.scalar_tensor_tensor(
-                    out=dd[:, ob, :], in0=accs[ob][:], scalar=bcol, in1=e2[:, ob, :], op0=ALU.add, op1=ALU.mult
-                )
-            nc.vector.scalar_tensor_tensor(
-                out=dd[:], in0=z[:], scalar=qc(g, 1), in1=dd[:], op0=ALU.mult, op1=ALU.add
-            )
-            nc.vector.scalar_tensor_tensor(
-                out=nn[:], in0=z[:], scalar=pc(g, 2), in1=nn[:], op0=ALU.mult, op1=ALU.add
-            )
-
-        def mid(u):
-            dd = work[u][1]
-            nc.scalar.activation(out=dd[:], in_=dd[:], func=AF.Abs)
-            nc.scalar.activation(out=dd[:], in_=dd[:], func=AF.Abs_reciprocal_sqrt, bias=one[:], scale=1.0)
-
-        def back(u):
-            g, h = divmod(u, 2)
-            nn, dd = work[u]
-            rr = ep.tile([P, NBH, GOUT], F32, name="rr")
-            oo = ep.tile([P, NBH, GOUT], F32, name="oo")
-            for nb in range(NBH):
-                tw = tpp.tile([P, GOUT], F32, name="tw", tag="tp")
-                tn = tpp.tile([P, GOUT], F32, name="tn", tag="tp")
-                for ob in range(OB):
-                    nc.tensor.transpose(
-                        out=tw[:, ob * P : (ob + 1) * P], in_=dd[:, ob, nb * P : (nb + 1) * P], identity=ident[:]
-                    )
-                for ob in range(OB):
-                    nc.tensor.transpose(
-                        out=tn[:, ob * P : (ob + 1) * P], in_=nn[:, ob, nb * P : (nb + 1) * P], identity=ident[:]
-                    )
-                nc.scalar.activation(out=rr[:, nb, :], in_=tw[:], func=AF.Square)
-                nc.vector.scalar_tensor_tensor(
-                    out=oo[:, nb, :], in0=tn[:], scalar=pc(g, 0), in1=rr[:, nb, :], op0=ALU.add, op1=ALU.mult
-                )
-                r0 = h * HALF + nb * P
-                nc.sync.dma_start(out=out[r0 : r0 + P, g * GOUT : (g + 1) * GOUT], in_=oo[:, nb, :])
-
-        load(0)
-        load(1)
+        one = const.tile([P, 1], F32, name="one")
+        nc.vector.memset(one[:], 1.0)
+        warm = const.tile([P, 1], F32, name="warm")
+        nc.scalar.activation(out=warm[:], in_=one[:], func=AF.Abs_reciprocal_sqrt)
+        ident = const.tile([P, P], F32, name="ident")
+        make_identity(nc, ident[:])
 
         bzf = const.tile([P, P], F32, name="bzf")
         nc.vector.tensor_copy(out=bzf[:], in_=bz[:])
@@ -191,20 +60,216 @@ def tile_groupkanlayer_kernel(tc, x, W, b, p, q, out):
         def qc(g, j):
             return cf[:, 32 + 3 * g + j : 32 + 3 * g + j + 1]
 
-        prep_w(0)
-        prep_x(0, 0)
-        prep_x(0, 1)
+        def bc(g, ob):
+            return bT[:, g * OB + ob : g * OB + ob + 1]
+
         n_units = 2 * G
-        for u in range(n_units):
-            g, h = divmod(u, 2)
-            front(u)
-            if u >= 1:
-                back(u - 1)
-            mid(u)
-            if g + 1 < G:
+        t_xs, t_wt, t_gx, t_gw, t_xq, t_wq = {}, {}, {}, {}, {}, {}
+        t_acc, t_z, t_e, t_nd, t_ro, t_tw = {}, {}, {}, {}, {}, {}
+
+        def load(g):
+            xs = inp.tile([P, 2 * NBH, GIN], BF16, name="xs")
+            wt = inp.tile([P, 4, GOUT], BF16, name="wt")
+            t_xs[g], t_wt[g] = xs, wt
+            for h in range(2):
+                nc.sync.dma_start(
+                    out=xs[:, h * NBH : (h + 1) * NBH, :],
+                    in_=x[h * HALF : (h + 1) * HALF, g * GIN : (g + 1) * GIN].rearrange("(nb r) c -> r nb c", r=P),
+                )
                 if h == 0:
-                    if g + 2 < G:
-                        load(g + 2)
-                    prep_w(g + 1)
-                prep_x(g + 1, h)
-        back(n_units - 1)
+                    nc.sync.dma_start(
+                        out=wt[:].rearrange("k (u e) c -> k u (e c)", u=2),
+                        in_=W[g].rearrange("(u k e) c -> k u (e c)", u=2, e=2),
+                    )
+
+        def reg_w(s):
+            g, hw = divmod(s, 2)
+            if hw == 0:
+                t_gw[g] = grp.tile([P, GOUT, 4], BF16, name="gw", align_bytes=64)
+            cols = slice(hw * 256, (hw + 1) * 256)
+            nc.scalar.copy(
+                out=t_gw[g][:, cols, :].rearrange("k (c i) t -> k c t i", i=4),
+                in_=t_wt[g][:, :, cols].rearrange("k t (c i) -> k c t i", i=4),
+            )
+
+        def q_w(s):
+            g, hw = divmod(s, 2)
+            if hw == 0:
+                wq = qnt.tile([P, GOUT], U32, name="wq", align_bytes=64)
+                wsc = qnt.tile([P, GOUT], U8, name="wsc", align_bytes=64)
+                t_wq[g] = (wq, wsc)
+            wq, wsc = t_wq[g]
+            cols = slice(hw * 256, (hw + 1) * 256)
+            nc.vector.quantize_mx(
+                out=wq[:, cols].bitcast(FP8X4), scales=wsc[:, cols], in_=t_gw[g][:, cols, :].rearrange("k o t -> k (o t)")
+            )
+
+        def x_t(v):
+            g, h = divmod(v, 2)
+            if h == 0:
+                t_gx[g] = grp.tile([P, 4 * N_ROWS], BF16, name="gx", align_bytes=64)
+            xf = t_xs[g][:].bitcast(F32)
+            gxf = t_gx[g][:].bitcast(F32).rearrange("k (n u) -> k n u", u=2)
+            for j in range(2):
+                xt = tpp.tile([P, 2, 2 * P], F32, name="xt", tag="tp")
+                for k in range(2):
+                    nb = h * NBH + 2 * j + k
+                    for u in range(2):
+                        nc.tensor.transpose(
+                            out=xt[:, u, k * P : (k + 1) * P], in_=xf[:, nb, u * P : (u + 1) * P], identity=ident[:]
+                        )
+                n0 = h * HALF + j * 2 * P
+                nc.scalar.copy(out=gxf[:, n0 : n0 + 2 * P, :], in_=xt[:].rearrange("k u n -> k n u"))
+
+        def q_x(v):
+            g, h = divmod(v, 2)
+            if h == 0:
+                xq = qnt.tile([P, N_ROWS], U32, name="xq", align_bytes=64)
+                xsc = qnt.tile([P, N_ROWS], U8, name="xsc", align_bytes=64)
+                t_xq[g] = (xq, xsc)
+            xq, xsc = t_xq[g]
+            nc.vector.quantize_mx(
+                out=xq[:, h * HALF : (h + 1) * HALF].bitcast(FP8X4),
+                scales=xsc[:, h * HALF : (h + 1) * HALF],
+                in_=t_gx[g][:, h * 4 * HALF : (h + 1) * 4 * HALF],
+            )
+
+        def mx(u, ob):
+            g, h = divmod(u, 2)
+            xq, xsc = t_xq[g]
+            wq, wsc = t_wq[g]
+            acc = accp.tile([P, HALF], F32, name="acc")
+            t_acc[(u, ob)] = acc
+            nc.tensor.matmul_mx(
+                out=acc[:],
+                lhsT=wq[:, ob * P : (ob + 1) * P].bitcast(FP8X4),
+                lhsT_scale=wsc[:, ob * P : (ob + 1) * P],
+                rhs=xq[:, h * HALF : (h + 1) * HALF].bitcast(FP8X4),
+                rhs_scale=xsc[:, h * HALF : (h + 1) * HALF],
+                start=True,
+                stop=True,
+            )
+
+        def zz(u, ob):
+            g = u // 2
+            if ob == 0:
+                t_z[u] = ep.tile([P, OB, HALF], F32, name="z")
+            nc.scalar.activation(out=t_z[u][:, ob, :], in_=t_acc[(u, ob)][:], func=AF.Square, bias=bc(g, ob), scale=1.0)
+
+        def ee(u, j):
+            g = u // 2
+            if j == 0:
+                e1 = ep.tile([P, OB, HALF], F32, name="e1")
+                e2 = ep.tile([P, OB, HALF], F32, name="e2")
+                t_e[u] = (e1, e2)
+            e1, e2 = t_e[u]
+            z = t_z[u]
+            s = slice(2 * j, 2 * j + 2)
+            nc.gpsimd.tensor_scalar(
+                out=e1[:, s, :], in0=z[:, s, :], scalar1=pc(g, 3), scalar2=pc(g, 1), op0=ALU.mult, op1=ALU.add
+            )
+            nc.gpsimd.tensor_scalar(
+                out=e2[:, s, :], in0=z[:, s, :], scalar1=qc(g, 2), scalar2=qc(g, 0), op0=ALU.mult, op1=ALU.add
+            )
+
+        def ye(u, ob):
+            g = u // 2
+            if ob == 0:
+                nn = ep.tile([P, OB, HALF], F32, name="nn")
+                dd = ep.tile([P, OB, HALF], F32, name="dd")
+                t_nd[u] = (nn, dd)
+            nn, dd = t_nd[u]
+            e1, e2 = t_e[u]
+            acc = t_acc[(u, ob)]
+            nc.vector.scalar_tensor_tensor(
+                out=dd[:, ob, :], in0=acc[:], scalar=bc(g, ob), in1=e2[:, ob, :], op0=ALU.add, op1=ALU.mult
+            )
+            nc.vector.scalar_tensor_tensor(
+                out=nn[:, ob, :], in0=acc[:], scalar=bc(g, ob), in1=e1[:, ob, :], op0=ALU.add, op1=ALU.mult
+            )
+
+        def dn(u):
+            g = u // 2
+            nn, dd = t_nd[u]
+            z = t_z[u]
+            nc.vector.scalar_tensor_tensor(out=dd[:], in0=z[:], scalar=qc(g, 1), in1=dd[:], op0=ALU.mult, op1=ALU.add)
+            nc.vector.scalar_tensor_tensor(out=nn[:], in0=z[:], scalar=pc(g, 2), in1=nn[:], op0=ALU.mult, op1=ALU.add)
+
+        def ab(u, a):
+            v = t_nd[u][1][:, :, a * 256 : (a + 1) * 256]
+            nc.scalar.activation(out=v, in_=v, func=AF.Abs)
+
+        def ars(u, a):
+            v = t_nd[u][1][:, :, a * 256 : (a + 1) * 256]
+            nc.scalar.activation(out=v, in_=v, func=AF.Abs_reciprocal_sqrt, bias=one[:], scale=1.0)
+
+        def t_w(u, nb):
+            dd = t_nd[u][1]
+            tw = tpp.tile([P, GOUT], F32, name="tw", tag="tp")
+            t_tw[(u, nb)] = tw
+            for ob in range(OB):
+                nc.tensor.transpose(
+                    out=tw[:, ob * P : (ob + 1) * P], in_=dd[:, ob, nb * P : (nb + 1) * P], identity=ident[:]
+                )
+
+        def sq(u, nb):
+            if nb == 0:
+                rr = ep.tile([P, NBH, GOUT], F32, name="rr")
+                oo = ep.tile([P, NBH, GOUT], F32, name="oo")
+                t_ro[u] = (rr, oo)
+            nc.scalar.activation(out=t_ro[u][0][:, nb, :], in_=t_tw[(u, nb)][:], func=AF.Square)
+
+        def fin(u, nb):
+            g, h = divmod(u, 2)
+            nn = t_nd[u][0]
+            rr, oo = t_ro[u]
+            tn = tpp.tile([P, GOUT], F32, name="tn", tag="tp")
+            for ob in range(OB):
+                nc.tensor.transpose(
+                    out=tn[:, ob * P : (ob + 1) * P], in_=nn[:, ob, nb * P : (nb + 1) * P], identity=ident[:]
+                )
+            nc.vector.scalar_tensor_tensor(
+                out=oo[:, nb, :], in0=tn[:], scalar=pc(g, 0), in1=rr[:, nb, :], op0=ALU.add, op1=ALU.mult
+            )
+            r0 = h * HALF + nb * P
+            nc.sync.dma_start(out=out[r0 : r0 + P, g * GOUT : (g + 1) * GOUT], in_=oo[:, nb, :])
+
+        def ok(u):
+            return 0 <= u < n_units
+
+        for u in range(-6, n_units + 1):
+            if ok(u - 1):
+                ab(u - 1, 0)
+                ab(u - 1, 1)
+            for half in range(2):
+                for ob in (2 * half, 2 * half + 1):
+                    if ok(u):
+                        ye(u, ob)
+                    if ok(u + 1):
+                        mx(u + 1, ob)
+                if ok(u + 1):
+                    zz(u + 1, 2 * half)
+                if ok(u - 1):
+                    ars(u - 1, half)
+                if ok(u + 1):
+                    zz(u + 1, 2 * half + 1)
+                    ee(u + 1, half)
+            if ok(u):
+                dn(u)
+            if ok(u - 1):
+                for nb in range(NBH):
+                    t_w(u - 1, nb)
+                for nb in range(NBH):
+                    sq(u - 1, nb)
+                for nb in range(NBH):
+                    fin(u - 1, nb)
+            if ok(u + 4):
+                reg_w(u + 4)
+            if ok(u + 3):
+                x_t(u + 3)
+            if ok(u + 2):
+                q_x(u + 2)
+            if ok(u + 3):
+                q_w(u + 3)
+            if (u + 6) % 2 == 0 and (u + 6) // 2 < G:
+                load((u + 6) // 2)

@@ -27,6 +27,7 @@ def tile_groupkanlayer_kernel(tc, x, W, b, p, q, out):
         grp = ctx.enter_context(tc.tile_pool(name="grp", bufs=2))
         qnt = ctx.enter_context(tc.tile_pool(name="qnt", bufs=2))
         ep = ctx.enter_context(tc.tile_pool(name="ep", bufs=2))
+        op = ctx.enter_context(tc.tile_pool(name="op", bufs=4))
         accp = ctx.enter_context(tc.psum_pool(name="accp", bufs=4))
         tpp = ctx.enter_context(tc.psum_pool(name="tpp", bufs=4))
 
@@ -64,8 +65,9 @@ def tile_groupkanlayer_kernel(tc, x, W, b, p, q, out):
             return bT[:, g * OB + ob : g * OB + ob + 1]
 
         n_units = 2 * G
+        NPE, DPE = True, False
         t_xs, t_wt, t_gx, t_gw, t_xq, t_wq = {}, {}, {}, {}, {}, {}
-        t_acc, t_z, t_e, t_nd, t_ro, t_tw = {}, {}, {}, {}, {}, {}
+        t_acc, t_z, t_e, t_nd, t_rr, t_tw, t_aa, t_bq = {}, {}, {}, {}, {}, {}, {}, {}
 
         def load(g):
             xs = inp.tile([P, 2 * NBH, GIN], BF16, name="xs")
@@ -82,15 +84,17 @@ def tile_groupkanlayer_kernel(tc, x, W, b, p, q, out):
                         in_=W[g].rearrange("(u k e) c -> k u (e c)", u=2, e=2),
                     )
 
-        def reg_w(s):
+        def reg_w(s, eng):
             g, hw = divmod(s, 2)
             if hw == 0:
                 t_gw[g] = grp.tile([P, GOUT, 4], BF16, name="gw", align_bytes=64)
             cols = slice(hw * 256, (hw + 1) * 256)
-            nc.scalar.copy(
-                out=t_gw[g][:, cols, :].rearrange("k (c i) t -> k c t i", i=4),
-                in_=t_wt[g][:, :, cols].rearrange("k t (c i) -> k c t i", i=4),
-            )
+            dst = t_gw[g][:, cols, :].rearrange("k (c i) t -> k c t i", i=4)
+            src = t_wt[g][:, :, cols].rearrange("k t (c i) -> k c t i", i=4)
+            if eng == "act":
+                nc.scalar.copy(out=dst, in_=src)
+            else:
+                nc.vector.tensor_copy(out=dst, in_=src)
 
         def q_w(s):
             g, hw = divmod(s, 2)
@@ -104,22 +108,24 @@ def tile_groupkanlayer_kernel(tc, x, W, b, p, q, out):
                 out=wq[:, cols].bitcast(FP8X4), scales=wsc[:, cols], in_=t_gw[g][:, cols, :].rearrange("k o t -> k (o t)")
             )
 
-        def x_t(v):
+        def x_t(v, j, eng):
             g, h = divmod(v, 2)
-            if h == 0:
+            if h == 0 and j == 0:
                 t_gx[g] = grp.tile([P, 4 * N_ROWS], BF16, name="gx", align_bytes=64)
             xf = t_xs[g][:].bitcast(F32)
             gxf = t_gx[g][:].bitcast(F32).rearrange("k (n u) -> k n u", u=2)
-            for j in range(2):
-                xt = tpp.tile([P, 2, 2 * P], F32, name="xt", tag="tp")
-                for k in range(2):
-                    nb = h * NBH + 2 * j + k
-                    for u in range(2):
-                        nc.tensor.transpose(
-                            out=xt[:, u, k * P : (k + 1) * P], in_=xf[:, nb, u * P : (u + 1) * P], identity=ident[:]
-                        )
-                n0 = h * HALF + j * 2 * P
+            xt = tpp.tile([P, 2, 2 * P], F32, name="xt", tag="tp")
+            for k in range(2):
+                nb = h * NBH + 2 * j + k
+                for u in range(2):
+                    nc.tensor.transpose(
+                        out=xt[:, u, k * P : (k + 1) * P], in_=xf[:, nb, u * P : (u + 1) * P], identity=ident[:]
+                    )
+            n0 = h * HALF + j * 2 * P
+            if eng == "act":
                 nc.scalar.copy(out=gxf[:, n0 : n0 + 2 * P, :], in_=xt[:].rearrange("k u n -> k n u"))
+            else:
+                nc.vector.tensor_copy(out=gxf[:, n0 : n0 + 2 * P, :], in_=xt[:].rearrange("k u n -> k n u"))
 
         def q_x(v):
             g, h = divmod(v, 2)
@@ -166,17 +172,31 @@ def tile_groupkanlayer_kernel(tc, x, W, b, p, q, out):
             z = t_z[u]
             s = slice(2 * j, 2 * j + 2)
             nc.gpsimd.tensor_scalar(
-                out=e1[:, s, :], in0=z[:, s, :], scalar1=pc(g, 3), scalar2=pc(g, 1), op0=ALU.mult, op1=ALU.add
-            )
-            nc.gpsimd.tensor_scalar(
                 out=e2[:, s, :], in0=z[:, s, :], scalar1=qc(g, 2), scalar2=qc(g, 0), op0=ALU.mult, op1=ALU.add
             )
+            nc.gpsimd.tensor_scalar(
+                out=e1[:, s, :], in0=z[:, s, :], scalar1=pc(g, 3), scalar2=pc(g, 1), op0=ALU.mult, op1=ALU.add
+            )
+
+        def mk_a(u):
+            g = u // 2
+            aa = ep.tile([P, OB, HALF], F32, name="aa", bufs=3)
+            t_aa[u] = aa
+            nc.gpsimd.tensor_scalar(
+                out=aa[:], in0=t_z[u][:], scalar1=pc(g, 2), scalar2=pc(g, 0), op0=ALU.mult, op1=ALU.add
+            )
+
+        def mk_b(u):
+            g = u // 2
+            bq = ep.tile([P, OB, HALF], F32, name="bq", bufs=2)
+            t_bq[u] = bq
+            nc.vector.tensor_scalar(out=bq[:], in0=t_z[u][:], scalar1=qc(g, 1), scalar2=None, op0=ALU.mult)
 
         def ye(u, ob):
             g = u // 2
             if ob == 0:
-                nn = ep.tile([P, OB, HALF], F32, name="nn")
-                dd = ep.tile([P, OB, HALF], F32, name="dd")
+                nn = ep.tile([P, OB, HALF], F32, name="nn", bufs=3)
+                dd = ep.tile([P, OB, HALF], F32, name="dd", bufs=3)
                 t_nd[u] = (nn, dd)
             nn, dd = t_nd[u]
             e1, e2 = t_e[u]
@@ -188,19 +208,16 @@ def tile_groupkanlayer_kernel(tc, x, W, b, p, q, out):
                 out=nn[:, ob, :], in0=acc[:], scalar=bc(g, ob), in1=e1[:, ob, :], op0=ALU.add, op1=ALU.mult
             )
 
-        def dn(u):
+        def d_add(u, ob):
             g = u // 2
-            nn, dd = t_nd[u]
-            z = t_z[u]
-            nc.vector.scalar_tensor_tensor(out=dd[:], in0=z[:], scalar=qc(g, 1), in1=dd[:], op0=ALU.mult, op1=ALU.add)
-            nc.vector.scalar_tensor_tensor(out=nn[:], in0=z[:], scalar=pc(g, 2), in1=nn[:], op0=ALU.mult, op1=ALU.add)
+            dd = t_nd[u][1]
+            nc.vector.scalar_tensor_tensor(
+                out=dd[:, ob, :], in0=t_z[u][:, ob, :], scalar=qc(g, 1), in1=dd[:, ob, :], op0=ALU.mult, op1=ALU.add
+            )
 
-        def ab(u, a):
-            v = t_nd[u][1][:, :, a * 256 : (a + 1) * 256]
+        def ab_ars(u, ob):
+            v = t_nd[u][1][:, ob, :]
             nc.scalar.activation(out=v, in_=v, func=AF.Abs)
-
-        def ars(u, a):
-            v = t_nd[u][1][:, :, a * 256 : (a + 1) * 256]
             nc.scalar.activation(out=v, in_=v, func=AF.Abs_reciprocal_sqrt, bias=one[:], scale=1.0)
 
         def t_w(u, nb):
@@ -214,62 +231,66 @@ def tile_groupkanlayer_kernel(tc, x, W, b, p, q, out):
 
         def sq(u, nb):
             if nb == 0:
-                rr = ep.tile([P, NBH, GOUT], F32, name="rr")
-                oo = ep.tile([P, NBH, GOUT], F32, name="oo")
-                t_ro[u] = (rr, oo)
-            nc.scalar.activation(out=t_ro[u][0][:, nb, :], in_=t_tw[(u, nb)][:], func=AF.Square)
+                t_rr[u] = ep.tile([P, NBH, GOUT], F32, name="rr", bufs=2)
+            nc.scalar.activation(out=t_rr[u][:, nb, :], in_=t_tw[(u, nb)][:], func=AF.Square)
+
+        def t_n(u, nb):
+            nn = t_nd[u][0]
+            aa = t_aa[u]
+            tn = tpp.tile([P, GOUT], F32, name="tn", tag="tp")
+            t_tw[(u, nb, 1)] = tn
+            for ob in range(OB):
+                nc.tensor.matmul(
+                    out=tn[:, ob * P : (ob + 1) * P],
+                    lhsT=nn[:, ob, nb * P : (nb + 1) * P],
+                    rhs=ident[:],
+                    is_transpose=True,
+                    start=True,
+                    stop=False,
+                )
+                nc.tensor.matmul(
+                    out=tn[:, ob * P : (ob + 1) * P],
+                    lhsT=aa[:, ob, nb * P : (nb + 1) * P],
+                    rhs=ident[:],
+                    is_transpose=True,
+                    start=False,
+                    stop=True,
+                )
 
         def fin(u, nb):
             g, h = divmod(u, 2)
-            nn = t_nd[u][0]
-            rr, oo = t_ro[u]
-            tn = tpp.tile([P, GOUT], F32, name="tn", tag="tp")
-            for ob in range(OB):
-                nc.tensor.transpose(
-                    out=tn[:, ob * P : (ob + 1) * P], in_=nn[:, ob, nb * P : (nb + 1) * P], identity=ident[:]
-                )
-            nc.vector.scalar_tensor_tensor(
-                out=oo[:, nb, :], in0=tn[:], scalar=pc(g, 0), in1=rr[:, nb, :], op0=ALU.add, op1=ALU.mult
-            )
+            oo = op.tile([P, GOUT], F32, name="oo")
+            nc.vector.tensor_tensor(out=oo[:], in0=t_tw[(u, nb, 1)][:], in1=t_rr[u][:, nb, :], op=ALU.mult)
             r0 = h * HALF + nb * P
-            nc.sync.dma_start(out=out[r0 : r0 + P, g * GOUT : (g + 1) * GOUT], in_=oo[:, nb, :])
+            nc.sync.dma_start(out=out[r0 : r0 + P, g * GOUT : (g + 1) * GOUT], in_=oo[:])
 
-        def ok(u):
-            return 0 <= u < n_units
+        n_q = 4 * n_units
 
-        for u in range(-6, n_units + 1):
-            if ok(u - 1):
-                ab(u - 1, 0)
-                ab(u - 1, 1)
-            for half in range(2):
-                for ob in (2 * half, 2 * half + 1):
-                    if ok(u):
-                        ye(u, ob)
-                    if ok(u + 1):
-                        mx(u + 1, ob)
-                if ok(u + 1):
-                    zz(u + 1, 2 * half)
-                if ok(u - 1):
-                    ars(u - 1, half)
-                if ok(u + 1):
-                    zz(u + 1, 2 * half + 1)
-                    ee(u + 1, half)
-            if ok(u):
-                dn(u)
-            if ok(u - 1):
-                for nb in range(NBH):
-                    t_w(u - 1, nb)
-                for nb in range(NBH):
-                    sq(u - 1, nb)
-                for nb in range(NBH):
-                    fin(u - 1, nb)
-            if ok(u + 4):
-                reg_w(u + 4)
-            if ok(u + 3):
-                x_t(u + 3)
-            if ok(u + 2):
-                q_x(u + 2)
-            if ok(u + 3):
-                q_w(u + 3)
-            if (u + 6) % 2 == 0 and (u + 6) // 2 < G:
-                load((u + 6) // 2)
+        def at(i, f):
+            if 0 <= i < n_q:
+                f(i // 4, i % 4)
+
+        for t in range(-20, n_q + 8):
+            at(t - 7, t_n)
+            at(t, ye)
+            at(t, d_add)
+            at(t - 7, fin)
+            at(t - 5, t_w)
+            at(t - 6, sq)
+            at(t - 1, ab_ars)
+            at(t + 3, zz)
+            if 0 <= t + 3 < n_q and (t + 3) % 2 == 1:
+                ee((t + 3) // 4, ((t + 3) % 4) // 2)
+                if (t + 3) % 4 == 3:
+                    mk_a((t + 3) // 4)
+            if (t + 11) % 2 == 0 and 0 <= (t + 11) // 4 < n_units:
+                x_t((t + 11) // 4, ((t + 11) % 4) // 2, "act")
+            at(t + 4, mx)
+            if (t + 6) % 4 == 0 and 0 <= (t + 6) // 4 < n_units:
+                q_x((t + 6) // 4)
+            if (t + 14) % 4 == 0 and 0 <= (t + 14) // 4 < n_units:
+                reg_w((t + 14) // 4, "dve")
+            if (t + 11) % 4 == 0 and 0 <= (t + 11) // 4 < n_units:
+                q_w((t + 11) // 4)
+            if (t + 20) % 8 == 0 and (t + 20) // 8 < G:
+                load((t + 20) // 8)

@@ -146,15 +146,16 @@ def tile_groupkanlayer_kernel(tc, x, W, b, p, q, out):
             wq, wsc = t_wq[g]
             acc = accp.tile([P, HALF], F32, name="acc")
             t_acc[(u, ob)] = acc
-            nc.tensor.matmul_mx(
-                out=acc[:],
-                lhsT=wq[:, ob * P : (ob + 1) * P].bitcast(FP8X4),
-                lhsT_scale=wsc[:, ob * P : (ob + 1) * P],
-                rhs=xq[:, h * HALF : (h + 1) * HALF].bitcast(FP8X4),
-                rhs_scale=xsc[:, h * HALF : (h + 1) * HALF],
-                start=True,
-                stop=True,
-            )
+            for rep in range(2):
+                nc.tensor.matmul_mx(
+                    out=acc[:],
+                    lhsT=wq[:, ob * P : (ob + 1) * P].bitcast(FP8X4),
+                    lhsT_scale=wsc[:, ob * P : (ob + 1) * P],
+                    rhs=xq[:, h * HALF : (h + 1) * HALF].bitcast(FP8X4),
+                    rhs_scale=xsc[:, h * HALF : (h + 1) * HALF],
+                    start=True,
+                    stop=True,
+                )
 
         def zz(u, ob):
             g = u // 2

@@ -35,10 +35,10 @@ def tile_groupkanlayer_kernel(tc, x, W, b, p, q, out):
 
         bz = const.tile([P, P], BF16, name="bz")
         nc.vector.memset(bz[:], 0.0)
-        nc.scalar.dma_start(out=bz[0 : G * OB, :], in_=b.rearrange("g (ob o) -> (g ob) o", o=P))
+        nc.sync.dma_start(out=bz[0 : G * OB, :], in_=b.rearrange("g (ob o) -> (g ob) o", o=P))
         pq = const.tile([P, 64], BF16, name="pq")
-        nc.scalar.dma_start(out=pq[:, 0:32], in_=p.rearrange("g c -> (g c)").partition_broadcast(P))
-        nc.scalar.dma_start(out=pq[:, 32:56], in_=q.rearrange("g c -> (g c)").partition_broadcast(P))
+        nc.sync.dma_start(out=pq[:, 0:32], in_=p.rearrange("g c -> (g c)").partition_broadcast(P))
+        nc.sync.dma_start(out=pq[:, 32:56], in_=q.rearrange("g c -> (g c)").partition_broadcast(P))
         one = const.tile([P, 1], F32, name="one")
         nc.vector.memset(one[:], 1.0)
         warm = const.tile([P, 1], F32, name="warm")
@@ -65,7 +65,7 @@ def tile_groupkanlayer_kernel(tc, x, W, b, p, q, out):
             return bT[:, g * OB + ob : g * OB + ob + 1]
 
         n_units = 2 * G
-        NPE, DPE = True, False
+        NPE, DPE = True, True
         t_xs, t_wt, t_gx, t_gw, t_xq, t_wq = {}, {}, {}, {}, {}, {}
         t_acc, t_z, t_e, t_nd, t_rr, t_tw, t_aa, t_bq = {}, {}, {}, {}, {}, {}, {}, {}
 
@@ -146,16 +146,15 @@ def tile_groupkanlayer_kernel(tc, x, W, b, p, q, out):
             wq, wsc = t_wq[g]
             acc = accp.tile([P, HALF], F32, name="acc")
             t_acc[(u, ob)] = acc
-            for rep in range(2):
-                nc.tensor.matmul_mx(
-                    out=acc[:],
-                    lhsT=wq[:, ob * P : (ob + 1) * P].bitcast(FP8X4),
-                    lhsT_scale=wsc[:, ob * P : (ob + 1) * P],
-                    rhs=xq[:, h * HALF : (h + 1) * HALF].bitcast(FP8X4),
-                    rhs_scale=xsc[:, h * HALF : (h + 1) * HALF],
-                    start=True,
-                    stop=True,
-                )
+            nc.tensor.matmul_mx(
+                out=acc[:],
+                lhsT=wq[:, ob * P : (ob + 1) * P].bitcast(FP8X4),
+                lhsT_scale=wsc[:, ob * P : (ob + 1) * P],
+                rhs=xq[:, h * HALF : (h + 1) * HALF].bitcast(FP8X4),
+                rhs_scale=xsc[:, h * HALF : (h + 1) * HALF],
+                start=True,
+                stop=True,
+            )
 
         def zz(u, ob):
             g = u // 2
@@ -209,15 +208,13 @@ def tile_groupkanlayer_kernel(tc, x, W, b, p, q, out):
                 out=nn[:, ob, :], in0=acc[:], scalar=bc(g, ob), in1=e1[:, ob, :], op0=ALU.add, op1=ALU.mult
             )
 
-        def d_add(u, ob):
+        def d_add(u):
             g = u // 2
             dd = t_nd[u][1]
-            nc.vector.scalar_tensor_tensor(
-                out=dd[:, ob, :], in0=t_z[u][:, ob, :], scalar=qc(g, 1), in1=dd[:, ob, :], op0=ALU.mult, op1=ALU.add
-            )
+            nc.vector.scalar_tensor_tensor(out=dd[:], in0=t_z[u][:], scalar=qc(g, 1), in1=dd[:], op0=ALU.mult, op1=ALU.add)
 
-        def ab_ars(u, ob):
-            v = t_nd[u][1][:, ob, :]
+        def ab_ars(u, nb):
+            v = t_nd[u][1][:, :, nb * P : (nb + 1) * P]
             nc.scalar.activation(out=v, in_=v, func=AF.Abs)
             nc.scalar.activation(out=v, in_=v, func=AF.Abs_reciprocal_sqrt, bias=one[:], scale=1.0)
 
@@ -265,33 +262,74 @@ def tile_groupkanlayer_kernel(tc, x, W, b, p, q, out):
             r0 = h * HALF + nb * P
             nc.sync.dma_start(out=out[r0 : r0 + P, g * GOUT : (g + 1) * GOUT], in_=oo[:])
 
+        def t_d(u, nb):
+            dd = t_nd[u][1]
+            bq = t_bq[u]
+            td = tpp.tile([P, GOUT], F32, name="td", tag="tp")
+            t_tw[(u, nb)] = td
+            for ob in range(OB):
+                nc.tensor.matmul(
+                    out=td[:, ob * P : (ob + 1) * P],
+                    lhsT=dd[:, ob, nb * P : (nb + 1) * P],
+                    rhs=ident[:],
+                    is_transpose=True,
+                    start=True,
+                    stop=False,
+                )
+                nc.tensor.matmul(
+                    out=td[:, ob * P : (ob + 1) * P],
+                    lhsT=bq[:, ob, nb * P : (nb + 1) * P],
+                    rhs=ident[:],
+                    is_transpose=True,
+                    start=False,
+                    stop=True,
+                )
+
+        def recip(u, nb):
+            if nb == 0:
+                t_rr[u] = ep.tile([P, NBH, GOUT], F32, name="rr", bufs=2)
+            v = t_rr[u][:, nb, :]
+            nc.scalar.activation(out=v, in_=t_tw[(u, nb)][:], func=AF.Abs)
+            nc.scalar.activation(out=v, in_=v, func=AF.Abs_reciprocal_sqrt, bias=one[:], scale=1.0)
+            nc.scalar.activation(out=v, in_=v, func=AF.Square)
+
         n_q = 4 * n_units
 
         def at(i, f):
             if 0 <= i < n_q:
                 f(i // 4, i % 4)
 
+        def unit_at(t, off):
+            return (t - off) // 4 if (t - off) % 4 == 0 and 0 <= (t - off) // 4 < n_units else None
+
         for t in range(-20, n_q + 8):
-            at(t - 7, t_n)
+            at(t - 6, t_n)
             at(t, ye)
-            at(t, d_add)
-            at(t - 7, fin)
-            at(t - 5, t_w)
-            at(t - 6, sq)
-            at(t - 1, ab_ars)
-            at(t + 3, zz)
-            if 0 <= t + 3 < n_q and (t + 3) % 2 == 1:
-                ee((t + 3) // 4, ((t + 3) % 4) // 2)
-                if (t + 3) % 4 == 3:
-                    mk_a((t + 3) // 4)
+            at(t - 6, fin)
+            at(t - 4, t_d)
+            at(t - 5, recip)
             if (t + 11) % 2 == 0 and 0 <= (t + 11) // 4 < n_units:
                 x_t((t + 11) // 4, ((t + 11) % 4) // 2, "act")
-            at(t + 4, mx)
-            if (t + 6) % 4 == 0 and 0 <= (t + 6) // 4 < n_units:
-                q_x((t + 6) // 4)
-            if (t + 14) % 4 == 0 and 0 <= (t + 14) // 4 < n_units:
-                reg_w((t + 14) // 4, "dve")
-            if (t + 11) % 4 == 0 and 0 <= (t + 11) // 4 < n_units:
-                q_w((t + 11) // 4)
+            if t % 2 == 1 and 0 <= t + 3 < n_q:
+                at(t + 3, mx)
+                at(t + 4, mx)
+                at(t + 3, zz)
+                at(t + 4, zz)
+                ee((t + 4) // 4, ((t + 4) % 4) // 2)
+                if (t + 4) % 4 == 3:
+                    mk_a((t + 4) // 4)
+            if t % 4 == 3:
+                u = unit_at(t, 3)
+                if u is not None:
+                    mk_b(u)
+                u = unit_at(t, 3 - 8)
+                if u is not None:
+                    q_x(u)
+                u = unit_at(t, 3 - 12)
+                if u is not None:
+                    q_w(u)
+                u = unit_at(t, 3 - 16)
+                if u is not None:
+                    reg_w(u, "dve")
             if (t + 20) % 8 == 0 and (t + 20) // 8 < G:
                 load((t + 20) // 8)

@@ -65,9 +65,10 @@ def tile_groupkanlayer_kernel(tc, x, W, b, p, q, out):
             return bT[:, g * OB + ob : g * OB + ob + 1]
 
         n_units = 2 * G
-        NPE, DPE = True, True
+        NPE, DPE = True, False
         t_xs, t_wt, t_gx, t_gw, t_xq, t_wq = {}, {}, {}, {}, {}, {}
         t_acc, t_z, t_e, t_nd, t_rr, t_tw, t_aa, t_bq = {}, {}, {}, {}, {}, {}, {}, {}
+        t_yy = {}
 
         def load(g):
             xs = inp.tile([P, 2 * NBH, GIN], BF16, name="xs")
@@ -84,29 +85,17 @@ def tile_groupkanlayer_kernel(tc, x, W, b, p, q, out):
                         in_=W[g].rearrange("(u k e) c -> k u (e c)", u=2, e=2),
                     )
 
-        def reg_w(s, eng):
-            g, hw = divmod(s, 2)
-            if hw == 0:
-                t_gw[g] = grp.tile([P, GOUT, 4], BF16, name="gw", align_bytes=64)
-            cols = slice(hw * 256, (hw + 1) * 256)
-            dst = t_gw[g][:, cols, :].rearrange("k (c i) t -> k c t i", i=4)
-            src = t_wt[g][:, :, cols].rearrange("k t (c i) -> k c t i", i=4)
-            if eng == "act":
-                nc.scalar.copy(out=dst, in_=src)
-            else:
-                nc.vector.tensor_copy(out=dst, in_=src)
-
-        def q_w(s):
-            g, hw = divmod(s, 2)
-            if hw == 0:
-                wq = qnt.tile([P, GOUT], U32, name="wq", align_bytes=64)
-                wsc = qnt.tile([P, GOUT], U8, name="wsc", align_bytes=64)
-                t_wq[g] = (wq, wsc)
-            wq, wsc = t_wq[g]
-            cols = slice(hw * 256, (hw + 1) * 256)
-            nc.vector.quantize_mx(
-                out=wq[:, cols].bitcast(FP8X4), scales=wsc[:, cols], in_=t_gw[g][:, cols, :].rearrange("k o t -> k (o t)")
+        def reg_w(g):
+            t_gw[g] = grp.tile([P, GOUT, 4], BF16, name="gw", align_bytes=64)
+            nc.vector.tensor_copy(
+                out=t_gw[g][:].rearrange("k (c i) t -> k c t i", i=4), in_=t_wt[g][:].rearrange("k t (c i) -> k c t i", i=4)
             )
+
+        def q_w(g):
+            wq = qnt.tile([P, GOUT], U32, name="wq", align_bytes=64)
+            wsc = qnt.tile([P, GOUT], U8, name="wsc", align_bytes=64)
+            t_wq[g] = (wq, wsc)
+            nc.vector.quantize_mx(out=wq[:].bitcast(FP8X4), scales=wsc[:], in_=t_gw[g][:].rearrange("k o t -> k (o t)"))
 
         def x_t(v, j, eng):
             g, h = divmod(v, 2)
@@ -165,17 +154,15 @@ def tile_groupkanlayer_kernel(tc, x, W, b, p, q, out):
         def ee(u, j):
             g = u // 2
             if j == 0:
-                e1 = ep.tile([P, OB, HALF], F32, name="e1")
-                e2 = ep.tile([P, OB, HALF], F32, name="e2")
-                t_e[u] = (e1, e2)
-            e1, e2 = t_e[u]
+                t_e[u] = ep.tile([P, 2, OB, HALF], F32, name="e12")
+            e12 = t_e[u]
             z = t_z[u]
             s = slice(2 * j, 2 * j + 2)
             nc.gpsimd.tensor_scalar(
-                out=e2[:, s, :], in0=z[:, s, :], scalar1=qc(g, 2), scalar2=qc(g, 0), op0=ALU.mult, op1=ALU.add
+                out=e12[:, 0, s, :], in0=z[:, s, :], scalar1=qc(g, 2), scalar2=qc(g, 0), op0=ALU.mult, op1=ALU.add
             )
             nc.gpsimd.tensor_scalar(
-                out=e1[:, s, :], in0=z[:, s, :], scalar1=pc(g, 3), scalar2=pc(g, 1), op0=ALU.mult, op1=ALU.add
+                out=e12[:, 1, s, :], in0=z[:, s, :], scalar1=pc(g, 3), scalar2=pc(g, 1), op0=ALU.mult, op1=ALU.add
             )
 
         def mk_a(u):
@@ -195,26 +182,25 @@ def tile_groupkanlayer_kernel(tc, x, W, b, p, q, out):
         def ye(u, ob):
             g = u // 2
             if ob == 0:
-                nn = ep.tile([P, OB, HALF], F32, name="nn", bufs=3)
-                dd = ep.tile([P, OB, HALF], F32, name="dd", bufs=3)
-                t_nd[u] = (nn, dd)
-            nn, dd = t_nd[u]
-            e1, e2 = t_e[u]
-            acc = t_acc[(u, ob)]
+                yy = ep.tile([P, 2, OB, HALF], F32, name="yy", bufs=3)
+                t_nd[u] = (yy[:, 1], yy[:, 0])
+                t_yy[u] = yy
             nc.vector.scalar_tensor_tensor(
-                out=dd[:, ob, :], in0=acc[:], scalar=bc(g, ob), in1=e2[:, ob, :], op0=ALU.add, op1=ALU.mult
-            )
-            nc.vector.scalar_tensor_tensor(
-                out=nn[:, ob, :], in0=acc[:], scalar=bc(g, ob), in1=e1[:, ob, :], op0=ALU.add, op1=ALU.mult
+                out=t_yy[u][:, :, ob, :],
+                in0=t_acc[(u, ob)][:].unsqueeze(1).to_broadcast([P, 2, HALF]),
+                scalar=bc(g, ob),
+                in1=t_e[u][:, :, ob, :],
+                op0=ALU.add,
+                op1=ALU.mult,
             )
 
         def d_add(u):
             g = u // 2
             dd = t_nd[u][1]
-            nc.vector.scalar_tensor_tensor(out=dd[:], in0=t_z[u][:], scalar=qc(g, 1), in1=dd[:], op0=ALU.mult, op1=ALU.add)
+            nc.vector.scalar_tensor_tensor(out=dd, in0=t_z[u][:], scalar=qc(g, 1), in1=dd, op0=ALU.mult, op1=ALU.add)
 
-        def ab_ars(u, nb):
-            v = t_nd[u][1][:, :, nb * P : (nb + 1) * P]
+        def ab_ars(u, a):
+            v = t_nd[u][1][:, :, a * 2 * P : (a + 1) * 2 * P]
             nc.scalar.activation(out=v, in_=v, func=AF.Abs)
             nc.scalar.activation(out=v, in_=v, func=AF.Abs_reciprocal_sqrt, bias=one[:], scale=1.0)
 
@@ -302,12 +288,14 @@ def tile_groupkanlayer_kernel(tc, x, W, b, p, q, out):
         def unit_at(t, off):
             return (t - off) // 4 if (t - off) % 4 == 0 and 0 <= (t - off) // 4 < n_units else None
 
-        for t in range(-20, n_q + 8):
-            at(t - 6, t_n)
+        for t in range(-20, n_q + 12):
+            at(t - 8, t_n)
             at(t, ye)
-            at(t - 6, fin)
-            at(t - 4, t_d)
-            at(t - 5, recip)
+            at(t - 8, fin)
+            at(t - 6, t_w)
+            at(t - 7, sq)
+            if t % 2 == 0 and 0 <= t - 4 < n_q:
+                ab_ars((t - 4) // 4, ((t - 4) % 4) // 2)
             if (t + 11) % 2 == 0 and 0 <= (t + 11) // 4 < n_units:
                 x_t((t + 11) // 4, ((t + 11) % 4) // 2, "act")
             if t % 2 == 1 and 0 <= t + 3 < n_q:
@@ -321,15 +309,13 @@ def tile_groupkanlayer_kernel(tc, x, W, b, p, q, out):
             if t % 4 == 3:
                 u = unit_at(t, 3)
                 if u is not None:
-                    mk_b(u)
-                u = unit_at(t, 3 - 8)
+                    d_add(u)
+                u = unit_at(t, -5)
                 if u is not None:
                     q_x(u)
-                u = unit_at(t, 3 - 12)
-                if u is not None:
-                    q_w(u)
-                u = unit_at(t, 3 - 16)
-                if u is not None:
-                    reg_w(u, "dve")
+                if (t + 9) % 8 == 0 and 0 <= (t + 9) // 8 < G:
+                    q_w((t + 9) // 8)
+                if (t + 13) % 8 == 0 and 0 <= (t + 13) // 8 < G:
+                    reg_w((t + 13) // 8)
             if (t + 20) % 8 == 0 and (t + 20) // 8 < G:
                 load((t + 20) // 8)

@@ -64,6 +64,16 @@ def tile_groupkanlayer_kernel(tc, x, W, b, p, q, out):
         def bc(g, ob):
             return bT[:, g * OB + ob : g * OB + ob + 1]
 
+        cq = const.tile([P, G * OB], F32, name="cq")
+        for g in range(G):
+            nc.vector.tensor_scalar(
+                out=cq[:, g * OB : (g + 1) * OB],
+                in0=bT[:, g * OB : (g + 1) * OB],
+                scalar1=qc(g, 1),
+                scalar2=qc(g, 0),
+                op0=ALU.mult,
+                op1=ALU.add,
+            )
         n_units = 2 * G
         NPE, DPE = True, False
         t_xs, t_wt, t_gx, t_gw, t_xq, t_wq = {}, {}, {}, {}, {}, {}
@@ -158,9 +168,15 @@ def tile_groupkanlayer_kernel(tc, x, W, b, p, q, out):
             e12 = t_e[u]
             z = t_z[u]
             s = slice(2 * j, 2 * j + 2)
-            nc.gpsimd.tensor_scalar(
-                out=e12[:, 0, s, :], in0=z[:, s, :], scalar1=qc(g, 2), scalar2=qc(g, 0), op0=ALU.mult, op1=ALU.add
-            )
+            for ob in (2 * j, 2 * j + 1):
+                nc.gpsimd.tensor_scalar(
+                    out=e12[:, 0, ob, :],
+                    in0=z[:, ob, :],
+                    scalar1=qc(g, 2),
+                    scalar2=cq[:, g * OB + ob : g * OB + ob + 1],
+                    op0=ALU.mult,
+                    op1=ALU.add,
+                )
             nc.gpsimd.tensor_scalar(
                 out=e12[:, 1, s, :], in0=z[:, s, :], scalar1=pc(g, 3), scalar2=pc(g, 1), op0=ALU.mult, op1=ALU.add
             )
@@ -178,6 +194,16 @@ def tile_groupkanlayer_kernel(tc, x, W, b, p, q, out):
             bq = ep.tile([P, OB, HALF], F32, name="bq", bufs=2)
             t_bq[u] = bq
             nc.vector.tensor_scalar(out=bq[:], in0=t_z[u][:], scalar1=qc(g, 1), scalar2=None, op0=ALU.mult)
+
+        def ff(u, ob):
+            nc.vector.scalar_tensor_tensor(
+                out=t_e[u][:, 0, ob, :],
+                in0=t_acc[(u, ob)][:],
+                scalar=qc(u // 2, 1),
+                in1=t_e[u][:, 0, ob, :],
+                op0=ALU.mult,
+                op1=ALU.add,
+            )
 
         def ye(u, ob):
             g = u // 2
@@ -291,6 +317,7 @@ def tile_groupkanlayer_kernel(tc, x, W, b, p, q, out):
         for t in range(-20, n_q + 12):
             at(t - 8, t_n)
             at(t, ye)
+            at(t + 1, ff)
             at(t - 8, fin)
             at(t - 6, t_w)
             at(t - 7, sq)
@@ -307,9 +334,6 @@ def tile_groupkanlayer_kernel(tc, x, W, b, p, q, out):
                 if (t + 4) % 4 == 3:
                     mk_a((t + 4) // 4)
             if t % 4 == 3:
-                u = unit_at(t, 3)
-                if u is not None:
-                    d_add(u)
                 u = unit_at(t, -5)
                 if u is not None:
                     q_x(u)

@@ -181,12 +181,13 @@ def tile_groupkanlayer_kernel(tc, x, W, b, p, q, out):
                 out=e12[:, 1, s, :], in0=z[:, s, :], scalar1=pc(g, 3), scalar2=pc(g, 1), op0=ALU.mult, op1=ALU.add
             )
 
-        def mk_a(u):
+        def mk_a(u, j):
             g = u // 2
-            aa = ep.tile([P, OB, HALF], F32, name="aa", bufs=3)
-            t_aa[u] = aa
+            if j == 0:
+                t_aa[u] = ep.tile([P, OB, HALF], F32, name="aa", bufs=3)
+            s = slice(2 * j, 2 * j + 2)
             nc.gpsimd.tensor_scalar(
-                out=aa[:], in0=t_z[u][:], scalar1=pc(g, 2), scalar2=pc(g, 0), op0=ALU.mult, op1=ALU.add
+                out=t_aa[u][:, s, :], in0=t_z[u][:, s, :], scalar1=pc(g, 2), scalar2=pc(g, 0), op0=ALU.mult, op1=ALU.add
             )
 
         def mk_b(u):
@@ -226,17 +227,17 @@ def tile_groupkanlayer_kernel(tc, x, W, b, p, q, out):
             nc.vector.scalar_tensor_tensor(out=dd, in0=t_z[u][:], scalar=qc(g, 1), in1=dd, op0=ALU.mult, op1=ALU.add)
 
         def ab_ars(u, a):
-            v = t_nd[u][1][:, :, a * 2 * P : (a + 1) * 2 * P]
+            v = t_nd[u][1][:, 2 * a : 2 * a + 2, :]
             nc.scalar.activation(out=v, in_=v, func=AF.Abs)
             nc.scalar.activation(out=v, in_=v, func=AF.Abs_reciprocal_sqrt, bias=one[:], scale=1.0)
 
-        def t_w(u, nb):
+        def t_w(u, ob):
             dd = t_nd[u][1]
-            tw = tpp.tile([P, GOUT], F32, name="tw", tag="tp")
-            t_tw[(u, nb)] = tw
-            for ob in range(OB):
+            tw = tpp.tile([P, HALF], F32, name="tw", tag="tp")
+            t_tw[(u, ob)] = tw
+            for nb in range(NBH):
                 nc.tensor.transpose(
-                    out=tw[:, ob * P : (ob + 1) * P], in_=dd[:, ob, nb * P : (nb + 1) * P], identity=ident[:]
+                    out=tw[:, nb * P : (nb + 1) * P], in_=dd[:, ob, nb * P : (nb + 1) * P], identity=ident[:]
                 )
 
         def sq(u, nb):
@@ -244,14 +245,14 @@ def tile_groupkanlayer_kernel(tc, x, W, b, p, q, out):
                 t_rr[u] = ep.tile([P, NBH, GOUT], F32, name="rr", bufs=2)
             nc.scalar.activation(out=t_rr[u][:, nb, :], in_=t_tw[(u, nb)][:], func=AF.Square)
 
-        def t_n(u, nb):
+        def t_n(u, ob):
             nn = t_nd[u][0]
             aa = t_aa[u]
-            tn = tpp.tile([P, GOUT], F32, name="tn", tag="tp")
-            t_tw[(u, nb, 1)] = tn
-            for ob in range(OB):
+            tn = tpp.tile([P, HALF], F32, name="tn", tag="tp")
+            t_tw[(u, ob, 1)] = tn
+            for nb in range(NBH):
                 nc.tensor.matmul(
-                    out=tn[:, ob * P : (ob + 1) * P],
+                    out=tn[:, nb * P : (nb + 1) * P],
                     lhsT=nn[:, ob, nb * P : (nb + 1) * P],
                     rhs=ident[:],
                     is_transpose=True,
@@ -259,7 +260,7 @@ def tile_groupkanlayer_kernel(tc, x, W, b, p, q, out):
                     stop=False,
                 )
                 nc.tensor.matmul(
-                    out=tn[:, ob * P : (ob + 1) * P],
+                    out=tn[:, nb * P : (nb + 1) * P],
                     lhsT=aa[:, ob, nb * P : (nb + 1) * P],
                     rhs=ident[:],
                     is_transpose=True,
@@ -267,12 +268,16 @@ def tile_groupkanlayer_kernel(tc, x, W, b, p, q, out):
                     stop=True,
                 )
 
-        def fin(u, nb):
+        def fin(u, ob):
             g, h = divmod(u, 2)
-            oo = op.tile([P, GOUT], F32, name="oo")
-            nc.vector.tensor_tensor(out=oo[:], in0=t_tw[(u, nb, 1)][:], in1=t_rr[u][:, nb, :], op=ALU.mult)
-            r0 = h * HALF + nb * P
-            nc.sync.dma_start(out=out[r0 : r0 + P, g * GOUT : (g + 1) * GOUT], in_=oo[:])
+            oo = op.tile([P, NBH, P], F32, name="oo")
+            nc.vector.tensor_tensor(
+                out=oo[:].rearrange("r nb c -> r (nb c)"), in0=t_tw[(u, ob, 1)][:], in1=t_rr[u][:, ob, :], op=ALU.mult
+            )
+            c0 = g * GOUT + ob * P
+            nc.sync.dma_start(
+                out=out[h * HALF : (h + 1) * HALF, c0 : c0 + P].rearrange("(nb r) c -> r nb c", r=P), in_=oo[:]
+            )
 
         def t_d(u, nb):
             dd = t_nd[u][1]
@@ -315,14 +320,14 @@ def tile_groupkanlayer_kernel(tc, x, W, b, p, q, out):
             return (t - off) // 4 if (t - off) % 4 == 0 and 0 <= (t - off) // 4 < n_units else None
 
         for t in range(-20, n_q + 12):
-            at(t - 8, t_n)
+            at(t - 6, t_n)
             at(t, ye)
             at(t + 1, ff)
-            at(t - 8, fin)
-            at(t - 6, t_w)
-            at(t - 7, sq)
-            if t % 2 == 0 and 0 <= t - 4 < n_q:
-                ab_ars((t - 4) // 4, ((t - 4) % 4) // 2)
+            at(t - 6, fin)
+            at(t - 4, t_w)
+            at(t - 5, sq)
+            if t % 2 == 0 and 0 <= t - 2 < n_q:
+                ab_ars((t - 2) // 4, ((t - 2) % 4) // 2)
             if (t + 11) % 2 == 0 and 0 <= (t + 11) // 4 < n_units:
                 x_t((t + 11) // 4, ((t + 11) % 4) // 2, "act")
             if t % 2 == 1 and 0 <= t + 3 < n_q:
@@ -331,8 +336,7 @@ def tile_groupkanlayer_kernel(tc, x, W, b, p, q, out):
                 at(t + 3, zz)
                 at(t + 4, zz)
                 ee((t + 4) // 4, ((t + 4) % 4) // 2)
-                if (t + 4) % 4 == 3:
-                    mk_a((t + 4) // 4)
+                mk_a((t + 4) // 4, ((t + 4) % 4) // 2)
             if t % 4 == 3:
                 u = unit_at(t, -5)
                 if u is not None:

@@ -181,13 +181,12 @@ def tile_groupkanlayer_kernel(tc, x, W, b, p, q, out):
                 out=e12[:, 1, s, :], in0=z[:, s, :], scalar1=pc(g, 3), scalar2=pc(g, 1), op0=ALU.mult, op1=ALU.add
             )
 
-        def mk_a(u, j):
+        def mk_a(u):
             g = u // 2
-            if j == 0:
-                t_aa[u] = ep.tile([P, OB, HALF], F32, name="aa", bufs=3)
-            s = slice(2 * j, 2 * j + 2)
+            aa = ep.tile([P, OB, HALF], F32, name="aa", bufs=3)
+            t_aa[u] = aa
             nc.gpsimd.tensor_scalar(
-                out=t_aa[u][:, s, :], in0=t_z[u][:, s, :], scalar1=pc(g, 2), scalar2=pc(g, 0), op0=ALU.mult, op1=ALU.add
+                out=aa[:], in0=t_z[u][:], scalar1=pc(g, 2), scalar2=pc(g, 0), op0=ALU.mult, op1=ALU.add
             )
 
         def mk_b(u):
@@ -336,7 +335,8 @@ def tile_groupkanlayer_kernel(tc, x, W, b, p, q, out):
                 at(t + 3, zz)
                 at(t + 4, zz)
                 ee((t + 4) // 4, ((t + 4) % 4) // 2)
-                mk_a((t + 4) // 4, ((t + 4) % 4) // 2)
+                if (t + 4) % 4 == 3:
+                    mk_a((t + 4) // 4)
             if t % 4 == 3:
                 u = unit_at(t, -5)
                 if u is not None:

@@ -74,6 +74,9 @@ def tile_groupkanlayer_kernel(tc, x, W, b, p, q, out):
                 op0=ALU.mult,
                 op1=ALU.add,
             )
+        def where(u, k):
+            return u // 2, 2 * (u % 2) + k // 2, k % 2
+
         n_units = 2 * G
         NPE, DPE = True, False
         t_xs, t_wt, t_gx, t_gw, t_xq, t_wq = {}, {}, {}, {}, {}, {}
@@ -139,12 +142,12 @@ def tile_groupkanlayer_kernel(tc, x, W, b, p, q, out):
                 in_=t_gx[g][:, h * 4 * HALF : (h + 1) * 4 * HALF],
             )
 
-        def mx(u, ob):
-            g, h = divmod(u, 2)
+        def mx(u, k):
+            g, ob, h = where(u, k)
             xq, xsc = t_xq[g]
             wq, wsc = t_wq[g]
             acc = accp.tile([P, HALF], F32, name="acc")
-            t_acc[(u, ob)] = acc
+            t_acc[(u, k)] = acc
             nc.tensor.matmul_mx(
                 out=acc[:],
                 lhsT=wq[:, ob * P : (ob + 1) * P].bitcast(FP8X4),
@@ -155,11 +158,11 @@ def tile_groupkanlayer_kernel(tc, x, W, b, p, q, out):
                 stop=True,
             )
 
-        def zz(u, ob):
-            g = u // 2
-            if ob == 0:
+        def zz(u, k):
+            g, ob, h = where(u, k)
+            if k == 0:
                 t_z[u] = ep.tile([P, OB, HALF], F32, name="z")
-            nc.scalar.activation(out=t_z[u][:, ob, :], in_=t_acc[(u, ob)][:], func=AF.Square, bias=bc(g, ob), scale=1.0)
+            nc.scalar.activation(out=t_z[u][:, k, :], in_=t_acc[(u, k)][:], func=AF.Square, bias=bc(g, ob), scale=1.0)
 
         def ee(u, j):
             g = u // 2
@@ -168,15 +171,15 @@ def tile_groupkanlayer_kernel(tc, x, W, b, p, q, out):
             e12 = t_e[u]
             z = t_z[u]
             s = slice(2 * j, 2 * j + 2)
-            for ob in (2 * j, 2 * j + 1):
-                nc.gpsimd.tensor_scalar(
-                    out=e12[:, 0, ob, :],
-                    in0=z[:, ob, :],
-                    scalar1=qc(g, 2),
-                    scalar2=cq[:, g * OB + ob : g * OB + ob + 1],
-                    op0=ALU.mult,
-                    op1=ALU.add,
-                )
+            ob = where(u, 2 * j)[1]
+            nc.gpsimd.tensor_scalar(
+                out=e12[:, 0, s, :],
+                in0=z[:, s, :],
+                scalar1=qc(g, 2),
+                scalar2=cq[:, g * OB + ob : g * OB + ob + 1],
+                op0=ALU.mult,
+                op1=ALU.add,
+            )
             nc.gpsimd.tensor_scalar(
                 out=e12[:, 1, s, :], in0=z[:, s, :], scalar1=pc(g, 3), scalar2=pc(g, 1), op0=ALU.mult, op1=ALU.add
             )
@@ -205,17 +208,17 @@ def tile_groupkanlayer_kernel(tc, x, W, b, p, q, out):
                 op1=ALU.add,
             )
 
-        def ye(u, ob):
-            g = u // 2
-            if ob == 0:
+        def ye(u, k):
+            g, ob, h = where(u, k)
+            if k == 0:
                 yy = ep.tile([P, 2, OB, HALF], F32, name="yy", bufs=3)
                 t_nd[u] = (yy[:, 1], yy[:, 0])
                 t_yy[u] = yy
             nc.vector.scalar_tensor_tensor(
-                out=t_yy[u][:, :, ob, :],
-                in0=t_acc[(u, ob)][:].unsqueeze(1).to_broadcast([P, 2, HALF]),
+                out=t_yy[u][:, :, k, :],
+                in0=t_acc[(u, k)][:].unsqueeze(1).to_broadcast([P, 2, HALF]),
                 scalar=bc(g, ob),
-                in1=t_e[u][:, :, ob, :],
+                in1=t_e[u][:, :, k, :],
                 op0=ALU.add,
                 op1=ALU.mult,
             )
@@ -267,11 +270,11 @@ def tile_groupkanlayer_kernel(tc, x, W, b, p, q, out):
                     stop=True,
                 )
 
-        def fin(u, ob):
-            g, h = divmod(u, 2)
+        def fin(u, k):
+            g, ob, h = where(u, k)
             oo = op.tile([P, NBH, P], F32, name="oo")
             nc.vector.tensor_tensor(
-                out=oo[:].rearrange("r nb c -> r (nb c)"), in0=t_tw[(u, ob, 1)][:], in1=t_rr[u][:, ob, :], op=ALU.mult
+                out=oo[:].rearrange("r nb c -> r (nb c)"), in0=t_tw[(u, k, 1)][:], in1=t_rr[u][:, k, :], op=ALU.mult
             )
             c0 = g * GOUT + ob * P
             nc.sync.dma_start(
@@ -318,7 +321,7 @@ def tile_groupkanlayer_kernel(tc, x, W, b, p, q, out):
         def unit_at(t, off):
             return (t - off) // 4 if (t - off) % 4 == 0 and 0 <= (t - off) // 4 < n_units else None
 
-        for t in range(-20, n_q + 12):
+        for t in range(-22, n_q + 12):
             at(t - 6, t_n)
             at(t, ye)
             at(t + 1, ff)
@@ -327,8 +330,8 @@ def tile_groupkanlayer_kernel(tc, x, W, b, p, q, out):
             at(t - 5, sq)
             if t % 2 == 0 and 0 <= t - 2 < n_q:
                 ab_ars((t - 2) // 4, ((t - 2) % 4) // 2)
-            if (t + 11) % 2 == 0 and 0 <= (t + 11) // 4 < n_units:
-                x_t((t + 11) // 4, ((t + 11) % 4) // 2, "act")
+            if (t + 13) % 2 == 0 and 0 <= (t + 13) // 4 < n_units:
+                x_t((t + 13) // 4, ((t + 13) % 4) // 2, "act")
             if t % 2 == 1 and 0 <= t + 3 < n_q:
                 at(t + 3, mx)
                 at(t + 4, mx)
@@ -338,12 +341,12 @@ def tile_groupkanlayer_kernel(tc, x, W, b, p, q, out):
                 if (t + 4) % 4 == 3:
                     mk_a((t + 4) // 4)
             if t % 4 == 3:
-                u = unit_at(t, -5)
+                u = unit_at(t, -9)
                 if u is not None:
                     q_x(u)
                 if (t + 9) % 8 == 0 and 0 <= (t + 9) // 8 < G:
                     q_w((t + 9) // 8)
                 if (t + 13) % 8 == 0 and 0 <= (t + 13) // 8 < G:
                     reg_w((t + 13) // 8)
-            if (t + 20) % 8 == 0 and (t + 20) // 8 < G:
-                load((t + 20) // 8)
+            if (t + 22) % 8 == 0 and (t + 22) // 8 < G:
+                load((t + 22) // 8)

@@ -331,7 +331,7 @@ def tile_groupkanlayer_kernel(tc, x, W, b, p, q, out):
             if t % 2 == 0 and 0 <= t - 2 < n_q:
                 ab_ars((t - 2) // 4, ((t - 2) % 4) // 2)
             if (t + 13) % 2 == 0 and 0 <= (t + 13) // 4 < n_units:
-                x_t((t + 13) // 4, ((t + 13) % 4) // 2, "act")
+                x_t((t + 13) // 4, ((t + 13) % 4) // 2, "dve" if ((t + 13) // 2) % 8 == 7 else "act")
             if t % 2 == 1 and 0 <= t + 3 < n_q:
                 at(t + 3, mx)
                 at(t + 4, mx)

from contextlib import ExitStack

import concourse.mybir as mybir
from concourse.masks import make_identity

F32 = mybir.dt.float32
BF16 = mybir.dt.bfloat16
U32 = mybir.dt.uint32
U8 = mybir.dt.uint8
FP8X4 = mybir.dt.float8_e4m3fn_x4
AF = mybir.ActivationFunctionType
ALU = mybir.AluOpType

P = 128
N_ROWS, G, GIN, GOUT = 1024, 8, 512, 512
HALF = 512
OB = GOUT // P
NBH = HALF // P
FLOPS = 2 * N_ROWS * G * GIN * GOUT


def tile_groupkanlayer_kernel(tc, x, W, b, p, q, out):
    nc = tc.nc
    with ExitStack() as ctx:
        const = ctx.enter_context(tc.tile_pool(name="const", bufs=1))
        inp = ctx.enter_context(tc.tile_pool(name="inp", bufs=2))
        grp = ctx.enter_context(tc.tile_pool(name="grp", bufs=2))
        qnt = ctx.enter_context(tc.tile_pool(name="qnt", bufs=2))
        ep = ctx.enter_context(tc.tile_pool(name="ep", bufs=2))
        op = ctx.enter_context(tc.tile_pool(name="op", bufs=4))
        accp = ctx.enter_context(tc.psum_pool(name="accp", bufs=4))
        tpp = ctx.enter_context(tc.psum_pool(name="tpp", bufs=4))

        ctx.enter_context(tc.manual_schedule())

        bz = const.tile([P, P], BF16, name="bz")
        nc.vector.memset(bz[:], 0.0)
        nc.sync.dma_start(out=bz[0 : G * OB, :], in_=b.rearrange("g (ob o) -> (g ob) o", o=P))
        pq = const.tile([P, 64], BF16, name="pq")
        nc.sync.dma_start(out=pq[:, 0:32], in_=p.rearrange("g c -> (g c)").partition_broadcast(P))
        nc.sync.dma_start(out=pq[:, 32:56], in_=q.rearrange("g c -> (g c)").partition_broadcast(P))
        one = const.tile([P, 1], F32, name="one")
        nc.vector.memset(one[:], 1.0)
        warm = const.tile([P, 1], F32, name="warm")
        nc.scalar.activation(out=warm[:], in_=one[:], func=AF.Abs_reciprocal_sqrt)
        ident = const.tile([P, P], F32, name="ident")
        make_identity(nc, ident[:])

        bzf = const.tile([P, P], F32, name="bzf")
        nc.vector.tensor_copy(out=bzf[:], in_=bz[:])
        bps = tpp.tile([P, GOUT], F32, name="bps", tag="tp")
        nc.tensor.transpose(out=bps[:, 0:P], in_=bzf[:], identity=ident[:])
        bT = const.tile([P, G * OB], F32, name="bT")
        nc.vector.tensor_copy(out=bT[:], in_=bps[:, 0 : G * OB])
        cf = const.tile([P, 56], F32, name="cf")
        nc.vector.tensor_copy(out=cf[:], in_=pq[:, 0:56])

        def pc(g, j):
            return cf[:, 4 * g + j : 4 * g + j + 1]

        def qc(g, j):
            return cf[:, 32 + 3 * g + j : 32 + 3 * g + j + 1]

        def bc(g, ob):
            return bT[:, g * OB + ob : g * OB + ob + 1]

        cq = const.tile([P, G * OB], F32, name="cq")
        for g in range(G):
            nc.vector.tensor_scalar(
                out=cq[:, g * OB : (g + 1) * OB],
                in0=bT[:, g * OB : (g + 1) * OB],
                scalar1=qc(g, 1),
                scalar2=qc(g, 0),
                op0=ALU.mult,
                op1=ALU.add,
            )
        def where(u, k):
            return u // 2, 2 * (u % 2) + k // 2, k % 2

        n_units = 2 * G
        NPE, DPE = True, False
        t_xs, t_wt, t_gx, t_gw, t_xq, t_wq = {}, {}, {}, {}, {}, {}
        t_acc, t_z, t_e, t_nd, t_rr, t_tw, t_aa, t_bq = {}, {}, {}, {}, {}, {}, {}, {}
        t_yy = {}

        def load(g):
            xs = inp.tile([P, 2 * NBH, GIN], BF16, name="xs")
            wt = inp.tile([P, 4, GOUT], BF16, name="wt")
            t_xs[g], t_wt[g] = xs, wt
            for h in range(2):
                nc.sync.dma_start(
                    out=xs[:, h * NBH : (h + 1) * NBH, :],
                    in_=x[h * HALF : (h + 1) * HALF, g * GIN : (g + 1) * GIN].rearrange("(nb r) c -> r nb c", r=P),
                )
                if h == 0:
                    nc.sync.dma_start(
                        out=wt[:].rearrange("k (u e) c -> k u (e c)", u=2),
                        in_=W[g].rearrange("(u k e) c -> k u (e c)", u=2, e=2),
                    )

        def reg_w(g):
            t_gw[g] = grp.tile([P, GOUT, 4], BF16, name="gw", align_bytes=64)
            nc.vector.tensor_copy(
                out=t_gw[g][:].rearrange("k (c i) t -> k c t i", i=4), in_=t_wt[g][:].rearrange("k t (c i) -> k c t i", i=4)
            )

        def q_w(g):
            wq = qnt.tile([P, GOUT], U32, name="wq", align_bytes=64)
            wsc = qnt.tile([P, GOUT], U8, name="wsc", align_bytes=64)
            t_wq[g] = (wq, wsc)
            nc.vector.quantize_mx(out=wq[:].bitcast(FP8X4), scales=wsc[:], in_=t_gw[g][:].rearrange("k o t -> k (o t)"))

        def x_t(v, j, eng):
            g, h = divmod(v, 2)
            if h == 0 and j == 0:
                t_gx[g] = grp.tile([P, 4 * N_ROWS], BF16, name="gx", align_bytes=64)
            xf = t_xs[g][:].bitcast(F32)
            gxf = t_gx[g][:].bitcast(F32).rearrange("k (n u) -> k n u", u=2)
            xt = tpp.tile([P, 2, 2 * P], F32, name="xt", tag="tp")
            for k in range(2):
                nb = h * NBH + 2 * j + k
                for u in range(2):
                    nc.tensor.transpose(
                        out=xt[:, u, k * P : (k + 1) * P], in_=xf[:, nb, u * P : (u + 1) * P], identity=ident[:]
                    )
            n0 = h * HALF + j * 2 * P
            if eng == "act":
                nc.scalar.copy(out=gxf[:, n0 : n0 + 2 * P, :], in_=xt[:].rearrange("k u n -> k n u"))
            else:
                nc.vector.tensor_copy(out=gxf[:, n0 : n0 + 2 * P, :], in_=xt[:].rearrange("k u n -> k n u"))

        def q_x(v):
            g, h = divmod(v, 2)
            if h == 0:
                xq = qnt.tile([P, N_ROWS], U32, name="xq", align_bytes=64)
                xsc = qnt.tile([P, N_ROWS], U8, name="xsc", align_bytes=64)
                t_xq[g] = (xq, xsc)
            xq, xsc = t_xq[g]
            nc.vector.quantize_mx(
                out=xq[:, h * HALF : (h + 1) * HALF].bitcast(FP8X4),
                scales=xsc[:, h * HALF : (h + 1) * HALF],
                in_=t_gx[g][:, h * 4 * HALF : (h + 1) * 4 * HALF],
            )

        def mx(u, k):
            g, ob, h = where(u, k)
            xq, xsc = t_xq[g]
            wq, wsc = t_wq[g]
            acc = accp.tile([P, HALF], F32, name="acc")
            t_acc[(u, k)] = acc
            nc.tensor.matmul_mx(
                out=acc[:],
                lhsT=wq[:, ob * P : (ob + 1) * P].bitcast(FP8X4),
                lhsT_scale=wsc[:, ob * P : (ob + 1) * P],
                rhs=xq[:, h * HALF : (h + 1) * HALF].bitcast(FP8X4),
                rhs_scale=xsc[:, h * HALF : (h + 1) * HALF],
                start=True,
                stop=True,
            )

        def zz(u, k):
            g, ob, h = where(u, k)
            if k == 0:
                t_z[u] = ep.tile([P, OB, HALF], F32, name="z")
            nc.scalar.activation(out=t_z[u][:, k, :], in_=t_acc[(u, k)][:], func=AF.Square, bias=bc(g, ob), scale=1.0)

        def ee(u, j):
            g = u // 2
            if j == 0:
                t_e[u] = ep.tile([P, 2, OB, HALF], F32, name="e12")
            e12 = t_e[u]
            z = t_z[u]
            s = slice(2 * j, 2 * j + 2)
            ob = where(u, 2 * j)[1]
            nc.gpsimd.tensor_scalar(
                out=e12[:, 0, s, :],
                in0=z[:, s, :],
                scalar1=qc(g, 2),
                scalar2=cq[:, g * OB + ob : g * OB + ob + 1],
                op0=ALU.mult,
                op1=ALU.add,
            )
            nc.gpsimd.tensor_scalar(
                out=e12[:, 1, s, :], in0=z[:, s, :], scalar1=pc(g, 3), scalar2=pc(g, 1), op0=ALU.mult, op1=ALU.add
            )

        def mk_a(u):
            g = u // 2
            aa = ep.tile([P, OB, HALF], F32, name="aa", bufs=3)
            t_aa[u] = aa
            nc.gpsimd.tensor_scalar(
                out=aa[:], in0=t_z[u][:], scalar1=pc(g, 2), scalar2=pc(g, 0), op0=ALU.mult, op1=ALU.add
            )

        def mk_b(u):
            g = u // 2
            bq = ep.tile([P, OB, HALF], F32, name="bq", bufs=2)
            t_bq[u] = bq
            nc.vector.tensor_scalar(out=bq[:], in0=t_z[u][:], scalar1=qc(g, 1), scalar2=None, op0=ALU.mult)

        def ff(u, ob):
            nc.vector.scalar_tensor_tensor(
                out=t_e[u][:, 0, ob, :],
                in0=t_acc[(u, ob)][:],
                scalar=qc(u // 2, 1),
                in1=t_e[u][:, 0, ob, :],
                op0=ALU.mult,
                op1=ALU.add,
            )

        def ye(u, k):
            g, ob, h = where(u, k)
            if k == 0:
                yy = ep.tile([P, 2, OB, HALF], F32, name="yy", bufs=3)
                t_nd[u] = (yy[:, 1], yy[:, 0])
                t_yy[u] = yy
            nc.vector.scalar_tensor_tensor(
                out=t_yy[u][:, :, k, :],
                in0=t_acc[(u, k)][:].unsqueeze(1).to_broadcast([P, 2, HALF]),
                scalar=bc(g, ob),
                in1=t_e[u][:, :, k, :],
                op0=ALU.add,
                op1=ALU.mult,
            )

        def d_add(u):
            g = u // 2
            dd = t_nd[u][1]
            nc.vector.scalar_tensor_tensor(out=dd, in0=t_z[u][:], scalar=qc(g, 1), in1=dd, op0=ALU.mult, op1=ALU.add)

        def ab_ars(u, a):
            v = t_nd[u][1][:, 2 * a : 2 * a + 2, :]
            nc.scalar.activation(out=v, in_=v, func=AF.Abs)
            nc.scalar.activation(out=v, in_=v, func=AF.Abs_reciprocal_sqrt, bias=one[:], scale=1.0)

        def t_w(u, ob):
            dd = t_nd[u][1]
            tw = tpp.tile([P, HALF], F32, name="tw", tag="tp")
            t_tw[(u, ob)] = tw
            for nb in range(NBH):
                nc.tensor.transpose(
                    out=tw[:, nb * P : (nb + 1) * P], in_=dd[:, ob, nb * P : (nb + 1) * P], identity=ident[:]
                )

        def sq(u, nb):
            if nb == 0:
                t_rr[u] = ep.tile([P, NBH, GOUT], F32, name="rr", bufs=2)
            nc.scalar.activation(out=t_rr[u][:, nb, :], in_=t_tw[(u, nb)][:], func=AF.Square)

        def t_n(u, ob):
            nn = t_nd[u][0]
            aa = t_aa[u]
            tn = tpp.tile([P, HALF], F32, name="tn", tag="tp")
            t_tw[(u, ob, 1)] = tn
            for nb in range(NBH):
                nc.tensor.matmul(
                    out=tn[:, nb * P : (nb + 1) * P],
                    lhsT=nn[:, ob, nb * P : (nb + 1) * P],
                    rhs=ident[:],
                    is_transpose=True,
                    start=True,
                    stop=False,
                )
                nc.tensor.matmul(
                    out=tn[:, nb * P : (nb + 1) * P],
                    lhsT=aa[:, ob, nb * P : (nb + 1) * P],
                    rhs=ident[:],
                    is_transpose=True,
                    start=False,
                    stop=True,
                )

        def fin(u, k):
            g, ob, h = where(u, k)
            oo = op.tile([P, NBH, P], F32, name="oo")
            nc.vector.tensor_tensor(
                out=oo[:].rearrange("r nb c -> r (nb c)"), in0=t_tw[(u, k, 1)][:], in1=t_rr[u][:, k, :], op=ALU.mult
            )
            c0 = g * GOUT + ob * P
            nc.sync.dma_start(
                out=out[h * HALF : (h + 1) * HALF, c0 : c0 + P].rearrange("(nb r) c -> r nb c", r=P), in_=oo[:]
            )

        def t_d(u, nb):
            dd = t_nd[u][1]
            bq = t_bq[u]
            td = tpp.tile([P, GOUT], F32, name="td", tag="tp")
            t_tw[(u, nb)] = td
            for ob in range(OB):
                nc.tensor.matmul(
                    out=td[:, ob * P : (ob + 1) * P],
                    lhsT=dd[:, ob, nb * P : (nb + 1) * P],
                    rhs=ident[:],
                    is_transpose=True,
                    start=True,
                    stop=False,
                )
                nc.tensor.matmul(
                    out=td[:, ob * P : (ob + 1) * P],
                    lhsT=bq[:, ob, nb * P : (nb + 1) * P],
                    rhs=ident[:],
                    is_transpose=True,
                    start=False,
                    stop=True,
                )

        def recip(u, nb):
            if nb == 0:
                t_rr[u] = ep.tile([P, NBH, GOUT], F32, name="rr", bufs=2)
            v = t_rr[u][:, nb, :]
            nc.scalar.activation(out=v, in_=t_tw[(u, nb)][:], func=AF.Abs)
            nc.scalar.activation(out=v, in_=v, func=AF.Abs_reciprocal_sqrt, bias=one[:], scale=1.0)
            nc.scalar.activation(out=v, in_=v, func=AF.Square)

        n_q = 4 * n_units

        def at(i, f):
            if 0 <= i < n_q:
                f(i // 4, i % 4)

        def unit_at(t, off):
            return (t - off) // 4 if (t - off) % 4 == 0 and 0 <= (t - off) // 4 < n_units else None

        for t in range(-22, n_q + 12):
            at(t - 6, t_n)
            at(t, ye)
            at(t + 1, ff)
            at(t - 6, fin)
            at(t - 4, t_w)
            at(t - 5, sq)
            if t % 2 == 0 and 0 <= t - 2 < n_q:
                ab_ars((t - 2) // 4, ((t - 2) % 4) // 2)
            if (t + 13) % 2 == 0 and 0 <= (t + 13) // 4 < n_units:
                x_t((t + 13) // 4, ((t + 13) % 4) // 2, "dve" if ((t + 13) // 2) % 8 == 7 else "act")
            if t % 2 == 1 and 0 <= t + 3 < n_q:
                at(t + 3, mx)
                at(t + 4, mx)
                at(t + 3, zz)
                at(t + 4, zz)
                ee((t + 4) // 4, ((t + 4) % 4) // 2)
                if (t + 4) % 4 == 3:
                    mk_a((t + 4) // 4)
            if t % 4 == 3:
                u = unit_at(t, -9)
                if u is not None:
                    q_x(u)
                if (t + 9) % 8 == 0 and 0 <= (t + 9) // 8 < G:
                    q_w((t + 9) // 8)
                if (t + 13) % 8 == 0 and 0 <= (t + 13) // 8 < G:
                    reg_w((t + 13) // 8)
            if (t + 22) % 8 == 0 and (t + 22) // 8 < G:
                load((t + 22) // 8)
